import numpy as np
import ml_dtypes


def mxq(x, axis, fmt="e4m3"):
    dtype, down = {"e4m3": (ml_dtypes.float8_e4m3fn, 7), "e5m2": (ml_dtypes.float8_e5m2, 14)}[fmt]
    v = np.moveaxis(np.asarray(x, np.float32).astype(ml_dtypes.bfloat16).astype(np.float64), axis, -1)
    blocks = v.reshape(v.shape[:-1] + (-1, 32))
    amax = np.abs(blocks).max(-1, keepdims=True)
    byte = np.maximum(np.where(amax > 0, np.frexp(amax)[1] - 1 + 127, 0) - down, 1)
    scale = np.exp2(byte - 127.0)
    codes = (blocks / scale).astype(np.float32).astype(dtype).astype(np.float64)
    return np.moveaxis((codes * scale).reshape(v.shape), -1, axis)


WIDE = False


def mx_kscale(k):
    if not WIDE:
        return np.ones(k)
    levels = np.array([10, -10, 5, -5, 0])
    if k % 512:
        return np.exp2(np.random.permutation(np.resize(levels, k // 32))).repeat(32)
    a = np.empty((k // 512, 16))
    for p in range(k // 512):
        a[p, :8] = np.random.permutation(np.resize(levels, 8))
        for g in range(8):
            far = levels[np.abs(levels - a[p, g]) >= 10]
            a[p, g + 8] = far[np.random.randint(len(far))]
    return np.exp2(a.ravel()).repeat(32)


BF16 = ml_dtypes.bfloat16


def bf(x):
    return np.asarray(x, np.float32).astype(BF16)


def f64(x):
    return np.asarray(x).astype(np.float64)


B, Q, D = 4096, 128, 512
COMBOS = ((0, 1), (0, 2), (0, 3), (1, 0), (1, 2), (2, 0), (2, 1), (3, 0))
T = 0.07
V = 1 + max(max(c) for c in COMBOS)


def setup_inputs():
    s = mx_kscale(D)
    c = np.mean(s * s)
    shared = np.random.standard_normal((B, D))
    d = {}
    for v in range(V):
        gain = np.random.uniform(0.6, 1.6, (B, 1))
        own = np.random.standard_normal((B, D))
        d["x%d" % v] = bf((np.sqrt(0.1) * shared + np.sqrt(0.9) * own) * gain * s)
    for v in range(V):
        d["mem%d" % v] = bf(np.random.standard_normal((Q, D)) * c / s)
    return d


def reference(x0, x1, x2, x3, mem0, mem1, mem2, mem3):
    X = [f64(x0), f64(x1), f64(x2), f64(x3)]
    Mem = [f64(mem0), f64(mem1), f64(mem2), f64(mem3)]
    Xn = [np.sqrt(np.sum(x * x, axis=1, keepdims=True)) for x in X]
    Xq = [mxq(x, 1, "e4m3") for x in X]
    Mq = [mxq(m, 1, "e4m3") for m in Mem]
    outs = []
    for i, j in COMBOS:
        self_dot = np.sum(X[i] * X[j], axis=1, keepdims=True)
        mem_dot = Xq[i] @ Mq[j].T
        logits = np.concatenate([self_dot, mem_dot], axis=1)
        outs.append(np.exp(logits / (Xn[i] * Xn[j]) / T))
    return np.stack(outs)

@@ -1,0 +1,262 @@
+from contextlib import ExitStack
+
+import concourse.mybir as mybir
+from concourse.masks import make_identity
+
+BF16 = mybir.dt.bfloat16
+F32 = mybir.dt.float32
+U32 = mybir.dt.uint32
+U8 = mybir.dt.uint8
+FP8X4 = mybir.dt.float8_e4m3fn_x4
+ACT = mybir.ActivationFunctionType
+ALU = mybir.AluOpType
+
+P = 128
+B, Q, D = 4096, 128, 512
+V = 4
+NT = B // P
+TEMP = 0.07
+NCOMBO = 8
+ROW = Q + 1
+QUAD = 4
+OCT = 8
+LEAD = 6
+SCALAR_COPY_STEPS = frozenset([t for t in range(NT) if t % 4 == 1 or t >= NT - LEAD])
+PAIRS = ((0, 1), (0, 2), (0, 3), (1, 2))
+
+FLOPS = 2 * NCOMBO * B * ROW * D
+
+
+def tile_memorymoco_pa_t_kernel(tc, x0, x1, x2, x3, mem0, mem1, mem2, mem3, out):
+    nc = tc.nc
+    xs = (x0, x1, x2, x3)
+    mems = (mem0, mem1, mem2, mem3)
+    sqrt_temp = TEMP ** 0.5
+
+    with ExitStack() as ctx:
+        keep = ctx.enter_context(tc.tile_pool(name="keep", bufs=1))
+        opool = ctx.enter_context(tc.tile_pool(name="opool", bufs=2))
+        work = ctx.enter_context(tc.tile_pool(name="work", bufs=3))
+        junk = ctx.enter_context(tc.tile_pool(name="junk", bufs=2))
+        small = ctx.enter_context(tc.tile_pool(name="small", bufs=4))
+        psum = ctx.enter_context(tc.psum_pool(name="psum", bufs=2))
+        ctx.enter_context(tc.manual_schedule())
+
+        mem_nat = keep.tile([P, V, D], BF16, name="mem_nat")
+        for j in range(V):
+            nc.scalar.dma_start(out=mem_nat[:, j, :], in_=mems[j])
+        xt = {}
+        for q in range(NT // QUAD):
+            for v in range(V):
+                xq = keep.tile([P, QUAD, D], BF16, name="x%d_%d" % (v, q))
+                src = xs[v].rearrange("(p t) d -> p t d", t=NT)
+                xt[(v, q)] = xq
+                if q > 0:
+                    nc.sync.dma_start(out=xq[:], in_=src[:, QUAD * q:QUAD * q + QUAD, :])
+            if q == 0:
+                for half in range(2):
+                    for v in range(V):
+                        src = xs[v].rearrange("(p t) d -> p t d", t=NT)
+                        nc.sync.dma_start(out=xt[(v, 0)][:, 2 * half:2 * half + 2, :],
+                                          in_=src[:, 2 * half:2 * half + 2, :])
+
+        ident = keep.tile([P, P], F32, name="ident")
+        make_identity(nc, ident[:])
+        neg_half = keep.tile([P, V, QUAD], F32, name="neg_half")
+        nc.gpsimd.memset(neg_half[:], -0.5)
+        warm_in = keep.tile([P, 1], F32, name="warm_in")
+        warm_out = keep.tile([P, 1], F32, name="warm_out")
+        nc.vector.memset(warm_in[:], 0.0)
+        nc.scalar.activation(out=warm_out[:], in_=warm_in[:], func=ACT.Exp)
+
+        mem_codes = keep.tile([P, V * Q], U32, name="mem_codes", align_bytes=64)
+        mem_scales = keep.tile([P, V * Q], U8, name="mem_scales", align_bytes=64)
+
+        out_view = out.rearrange("c (p t) q -> p c (t q)", t=NT)
+
+        state = {}
+
+        def rows_of(v, t):
+            return xt[(v, t // QUAD)][:].bitcast(F32)[:, t % QUAD, :]
+
+        def transposes(key, sources):
+            banks = []
+            tpa = psum.tile([P, 2, 2, P], F32)
+            tpb = psum.tile([P, 2, 2, P], F32)
+            for n in range(V):
+                bank = tpa if n < 2 else tpb
+                for u in range(2):
+                    nc.tensor.transpose(bank[:, n % 2, u, :], sources[n][:, u:2 * P:2], ident[:])
+            banks.append(tpa)
+            banks.append(tpb)
+            state[("tp", key)] = banks
+
+        def copy_out(key):
+            banks = state.pop(("tp", key))
+            gt = work.tile([P, V, P, 4], BF16, align_bytes=64)
+            gtw = gt[:].bitcast(F32)
+            for h in range(2):
+                dst = gtw[:, 2 * h:2 * h + 2, :, :]
+                src = banks[h][:].rearrange("w n u p -> w n p u")
+                if h == 1 and key in SCALAR_COPY_STEPS:
+                    nc.scalar.copy(out=dst, in_=src)
+                else:
+                    nc.vector.tensor_copy(out=dst, in_=src)
+            state[("gt", key)] = gt
+
+        def quantise(key, codes, scales):
+            gt = state.pop(("gt", key))
+            nc.vector.quantize_mx(
+                out=codes[:].bitcast(FP8X4),
+                scales=scales[:],
+                in_=gt[:].rearrange("w n p j -> w (n p j)"),
+            )
+
+        def quantise_step(t):
+            codes = work.tile([P, V * P], U32, align_bytes=64)
+            scales = work.tile([P, V * P], U8, align_bytes=64)
+            quantise(t, codes, scales)
+            state[("cd", t)] = (codes, scales)
+
+        def mx_pass(dst, codes, scales, v, m_lo, m_hi):
+            nc.tensor.matmul_mx(
+                out=dst,
+                lhsT=codes[:, P * v:P * v + P].bitcast(FP8X4),
+                lhsT_scale=scales[:, P * v:P * v + P],
+                rhs=mem_codes[:, Q * m_lo:Q * m_hi].bitcast(FP8X4),
+                rhs_scale=mem_scales[:, Q * m_lo:Q * m_hi],
+                start=True,
+                stop=True,
+            )
+
+        def products(t):
+            codes, scales = state.pop(("cd", t))
+            ma = psum.tile([P, 4, Q], F32)
+            mb = psum.tile([P, 4, Q], F32)
+            maf = ma[:].rearrange("p n q -> p (n q)")
+            mx_pass(maf[:, 0:2 * Q], codes, scales, 0, 1, 3)
+            mx_pass(ma[:, 2, :], codes, scales, 1, 0, 1)
+            mx_pass(ma[:, 3, :], codes, scales, 2, 0, 1)
+            mx_pass(mb[:, 0, :], codes, scales, 0, 3, 4)
+            mx_pass(mb[:, 2, :], codes, scales, 1, 2, 3)
+            mx_pass(mb[:, 3, :], codes, scales, 2, 1, 2)
+            mx_pass(mb[:, 1, :], codes, scales, 3, 0, 1)
+            state[("mm", t)] = (ma, mb)
+
+        def exps(t):
+            ma, mb = state.pop(("mm", t))
+            ot = state[("o", t // OCT)]
+            sc = state[("s", t // QUAD)]
+            r = t % OCT
+            k = t % QUAD
+            nc.scalar.activation(out=ot[:, 1:6:4, r, 1:ROW], in_=ma[:, 1:4:2, :], func=ACT.Exp,
+                                 scale=sc[:, 1, k:k + 1])
+            nc.scalar.activation(out=ot[:, 0:4:3, r, 1:ROW], in_=ma[:, 0:3:2, :], func=ACT.Exp,
+                                 scale=sc[:, 0, k:k + 1])
+            nc.scalar.activation(out=ot[:, 2:8:5, r, 1:ROW], in_=mb[:, 0:2, :], func=ACT.Exp,
+                                 scale=sc[:, 2, k:k + 1])
+            nc.scalar.activation(out=ot[:, 4:7:2, r, 1:ROW], in_=mb[:, 2:4, :], func=ACT.Exp,
+                                 scale=sc[:, 3, k:k + 1])
+
+        def squares(t):
+            q, k = t // QUAD, t % QUAD
+            if k == 0:
+                n2 = small.tile([P, V, QUAD], F32)
+                state[("n2", q)] = n2
+            n2 = state[("n2", q)]
+            for v in range(V):
+                js = junk.tile([P, D], BF16)
+                nc.scalar.activation(out=js[:], in_=xt[(v, q)][:, k, :], func=ACT.Square,
+                                     scale=sqrt_temp, accum_out=n2[:, v, k:k + 1])
+
+        def dots(t):
+            q, k = t // QUAD, t % QUAD
+            if k == 0:
+                dt = small.tile([P, len(PAIRS), QUAD], F32)
+                state[("dt", q)] = dt
+            dt = state[("dt", q)]
+            for n, (i, j) in enumerate(PAIRS):
+                jv = junk.tile([P, D], BF16)
+                nc.vector.scalar_tensor_tensor(
+                    out=jv[:], in0=xt[(i, q)][:, k, :], scalar=1.0, in1=xt[(j, q)][:, k, :],
+                    op0=ALU.mult, op1=ALU.mult, accum_out=dt[:, n, k:k + 1],
+                )
+
+        def scales_of(q):
+            n2 = state.pop(("n2", q))
+            dt = state.pop(("dt", q))
+            rn = small.tile([P, V, QUAD], F32)
+            sc = small.tile([P, len(PAIRS), QUAD], F32)
+            zz = small.tile([P, len(PAIRS), QUAD], F32)
+            nc.gpsimd.tensor_tensor(out=rn[:], in0=n2[:], in1=neg_half[:], op=ALU.pow)
+            nc.gpsimd.tensor_tensor(out=sc[:, 0:3, :], in0=rn[:, 0:1, :].to_broadcast([P, 3, QUAD]),
+                                    in1=rn[:, 1:4, :], op=ALU.mult)
+            nc.gpsimd.tensor_tensor(out=sc[:, 3, :], in0=rn[:, 1, :], in1=rn[:, 2, :], op=ALU.mult)
+            nc.gpsimd.tensor_tensor(out=zz[:], in0=dt[:], in1=sc[:], op=ALU.mult)
+            state[("s", q)] = sc
+            state[("z", q)] = zz
+
+        def first_column(q):
+            if q % 2 == 0:
+                ot = opool.tile([P, NCOMBO, OCT, ROW], F32)
+                state[("o", q // 2)] = ot
+            ot = state[("o", q // 2)]
+            zz = state.pop(("z", q))
+            r = QUAD * (q % 2)
+            nc.scalar.activation(out=ot[:, 0:3, r:r + QUAD, 0], in_=zz[:, 0:3, :], func=ACT.Exp)
+            nc.scalar.activation(out=ot[:, 3:8:2, r:r + QUAD, 0], in_=zz[:, 0:3, :], func=ACT.Exp)
+            nc.scalar.activation(out=ot[:, 4:7:2, r:r + QUAD, 0],
+                                 in_=zz[:, 3:4, :].to_broadcast([P, 2, QUAD]), func=ACT.Exp)
+
+        def store(o, lo, hi):
+            ot = state[("o", o)]
+            base = o * OCT * ROW
+            nc.sync.dma_start(
+                out=out_view[:, :, base + lo:base + hi],
+                in_=ot[:].rearrange("p c t q -> p c (t q)")[:, :, lo:hi],
+            )
+
+        mem_words = mem_nat[:].bitcast(F32)
+        transposes("mem", [mem_words[:, j, :] for j in range(V)])
+
+        for t in range(LEAD):
+            squares(t)
+            dots(t)
+            if t == 1:
+                copy_out("mem")
+            if t == 2:
+                quantise("mem", mem_codes, mem_scales)
+            if t % QUAD == QUAD - 1:
+                scales_of(t // QUAD)
+
+        cuts = {}
+        for o in range(NT // OCT):
+            cuts[OCT * o + 3] = (o, 0, 512)
+            cuts[OCT * o + 7] = (o, 512, OCT * ROW)
+        last = NT // OCT - 1
+        cuts[OCT * last + 5] = (last, 512, 768)
+        cuts[OCT * last + 6] = (last, 768, 896)
+        cuts[OCT * last + 7] = (last, 896, OCT * ROW)
+
+        for i in range(-1, NT + 2):
+            if 0 <= i + 1 < NT:
+                transposes(i + 1, [rows_of(v, i + 1) for v in range(V)])
+            if 0 <= i < NT:
+                copy_out(i)
+            if 0 <= i - 1 < NT:
+                quantise_step(i - 1)
+                products(i - 1)
+            if 0 <= i - 2 < NT:
+                t = i - 2
+                if t % QUAD == 0:
+                    first_column(t // QUAD)
+                exps(t)
+                if t in cuts:
+                    o, lo, hi = cuts[t]
+                    store(o, lo, hi)
+            if i >= 0 and i + LEAD < NT:
+                t = i + LEAD
+                squares(t)
+                dots(t)
+                if t % QUAD == QUAD - 1:
+                    scales_of(t // QUAD)

@@ -7,6 +7,7 @@ BF16 = mybir.dt.bfloat16
 F32 = mybir.dt.float32
 U32 = mybir.dt.uint32
 U8 = mybir.dt.uint8
+I32 = mybir.dt.int32
 FP8X4 = mybir.dt.float8_e4m3fn_x4
 ACT = mybir.ActivationFunctionType
 ALU = mybir.AluOpType
@@ -23,6 +24,8 @@ OCT = 8
 LEAD = 6
 SCALAR_COPY_STEPS = frozenset([t for t in range(NT) if t % 4 == 1 or t >= NT - LEAD])
 PAIRS = ((0, 1), (0, 2), (0, 3), (1, 2))
+RSQRT_BITS = float(0x5F3759DF)
+NEWTON_STEPS = 3
 
 FLOPS = 2 * NCOMBO * B * ROW * D
 
@@ -62,8 +65,6 @@ def tile_memorymoco_pa_t_kernel(tc, x0, x1, x2, x3, mem0, mem1, mem2, mem3, out)
 
         ident = keep.tile([P, P], F32, name="ident")
         make_identity(nc, ident[:])
-        neg_half = keep.tile([P, V, QUAD], F32, name="neg_half")
-        nc.gpsimd.memset(neg_half[:], -0.5)
         warm_in = keep.tile([P, 1], F32, name="warm_in")
         warm_out = keep.tile([P, 1], F32, name="warm_out")
         nc.vector.memset(warm_in[:], 0.0)
@@ -185,13 +186,22 @@ def tile_memorymoco_pa_t_kernel(tc, x0, x1, x2, x3, mem0, mem1, mem2, mem3, out)
         def scales_of(q):
             n2 = state.pop(("n2", q))
             dt = state.pop(("dt", q))
-            rn = small.tile([P, V, QUAD], F32)
+            rn = small.tile([P, V, QUAD], I32)
+            nw = small.tile([P, V, QUAD], F32)
             sc = small.tile([P, len(PAIRS), QUAD], F32)
             zz = small.tile([P, len(PAIRS), QUAD], F32)
-            nc.gpsimd.tensor_tensor(out=rn[:], in0=n2[:], in1=neg_half[:], op=ALU.pow)
-            nc.gpsimd.tensor_tensor(out=sc[:, 0:3, :], in0=rn[:, 0:1, :].to_broadcast([P, 3, QUAD]),
-                                    in1=rn[:, 1:4, :], op=ALU.mult)
-            nc.gpsimd.tensor_tensor(out=sc[:, 3, :], in0=rn[:, 1, :], in1=rn[:, 2, :], op=ALU.mult)
+            nc.vector.tensor_scalar(out=rn[:], in0=n2[:].bitcast(I32), scalar1=-0.5, scalar2=RSQRT_BITS,
+                                    op0=ALU.mult, op1=ALU.add)
+            y = rn[:].bitcast(F32)
+            for step in range(NEWTON_STEPS):
+                nc.gpsimd.tensor_tensor(out=nw[:], in0=n2[:], in1=y, op=ALU.mult)
+                nc.gpsimd.tensor_tensor(out=nw[:], in0=nw[:], in1=y, op=ALU.mult)
+                nc.gpsimd.tensor_scalar(out=nw[:], in0=nw[:], scalar1=-0.5, scalar2=1.5,
+                                        op0=ALU.mult, op1=ALU.add)
+                nc.gpsimd.tensor_tensor(out=y, in0=nw[:], in1=y, op=ALU.mult)
+            nc.gpsimd.tensor_tensor(out=sc[:, 0:3, :], in0=y[:, 0:1, :].to_broadcast([P, 3, QUAD]),
+                                    in1=y[:, 1:4, :], op=ALU.mult)
+            nc.gpsimd.tensor_tensor(out=sc[:, 3, :], in0=y[:, 1, :], in1=y[:, 2, :], op=ALU.mult)
             nc.gpsimd.tensor_tensor(out=zz[:], in0=dt[:], in1=sc[:], op=ALU.mult)
             state[("s", q)] = sc
             state[("z", q)] = zz

@@ -21,8 +21,9 @@ NCOMBO = 8
 ROW = Q + 1
 QUAD = 4
 OCT = 8
-LEAD = 6
-SCALAR_COPY_STEPS = frozenset([t for t in range(NT) if t % 4 == 1 or t >= NT - LEAD])
+LEAD = 10
+DOTS_PER_STEP = 3
+SCALAR_COPY_FROM = NT - LEAD
 PAIRS = ((0, 1), (0, 2), (0, 3), (1, 2))
 RSQRT_BITS = float(0x5F3759DF)
 NEWTON_STEPS = 3
@@ -99,10 +100,11 @@ def tile_memorymoco_pa_t_kernel(tc, x0, x1, x2, x3, mem0, mem1, mem2, mem3, out)
             for h in range(2):
                 dst = gtw[:, 2 * h:2 * h + 2, :, :]
                 src = banks[h][:].rearrange("w n u p -> w n p u")
-                if h == 1 and key in SCALAR_COPY_STEPS:
+                if key != "mem" and key >= SCALAR_COPY_FROM:
                     nc.scalar.copy(out=dst, in_=src)
                 else:
                     nc.vector.tensor_copy(out=dst, in_=src)
+                    take_small()
             state[("gt", key)] = gt
 
         def quantise(key, codes, scales):
@@ -112,6 +114,7 @@ def tile_memorymoco_pa_t_kernel(tc, x0, x1, x2, x3, mem0, mem1, mem2, mem3, out)
                 scales=scales[:],
                 in_=gt[:].rearrange("w n p j -> w (n p j)"),
             )
+            take_small()
 
         def quantise_step(t):
             codes = work.tile([P, V * P], U32, align_bytes=64)
@@ -146,10 +149,13 @@ def tile_memorymoco_pa_t_kernel(tc, x0, x1, x2, x3, mem0, mem1, mem2, mem3, out)
 
         def exps(t):
             ma, mb = state.pop(("mm", t))
+            if t % OCT == 0:
+                ot = opool.tile([P, NCOMBO, OCT, ROW], F32)
+                state[("o", t // OCT)] = ot
             ot = state[("o", t // OCT)]
-            sc = state[("s", t // QUAD)]
+            sc = state[("s", t // OCT)]
             r = t % OCT
-            k = t % QUAD
+            k = r
             nc.scalar.activation(out=ot[:, 1:6:4, r, 1:ROW], in_=ma[:, 1:4:2, :], func=ACT.Exp,
                                  scale=sc[:, 1, k:k + 1])
             nc.scalar.activation(out=ot[:, 0:4:3, r, 1:ROW], in_=ma[:, 0:3:2, :], func=ACT.Exp,
@@ -160,63 +166,86 @@ def tile_memorymoco_pa_t_kernel(tc, x0, x1, x2, x3, mem0, mem1, mem2, mem3, out)
                                  scale=sc[:, 3, k:k + 1])
 
         def squares(t):
-            q, k = t // QUAD, t % QUAD
+            o, k = t // OCT, t % OCT
             if k == 0:
-                n2 = small.tile([P, V, QUAD], F32)
-                state[("n2", q)] = n2
-            n2 = state[("n2", q)]
+                n2 = small.tile([P, V, OCT], F32)
+                state[("n2", o)] = n2
+            n2 = state[("n2", o)]
             for v in range(V):
                 js = junk.tile([P, D], BF16)
-                nc.scalar.activation(out=js[:], in_=xt[(v, q)][:, k, :], func=ACT.Square,
+                nc.scalar.activation(out=js[:], in_=xt[(v, t // QUAD)][:, t % QUAD, :], func=ACT.Square,
                                      scale=sqrt_temp, accum_out=n2[:, v, k:k + 1])
 
-        def dots(t):
-            q, k = t // QUAD, t % QUAD
-            if k == 0:
-                dt = small.tile([P, len(PAIRS), QUAD], F32)
-                state[("dt", q)] = dt
-            dt = state[("dt", q)]
-            for n, (i, j) in enumerate(PAIRS):
-                jv = junk.tile([P, D], BF16)
-                nc.vector.scalar_tensor_tensor(
-                    out=jv[:], in0=xt[(i, q)][:, k, :], scalar=1.0, in1=xt[(j, q)][:, k, :],
-                    op0=ALU.mult, op1=ALU.mult, accum_out=dt[:, n, k:k + 1],
-                )
+        pending = []
 
-        def scales_of(q):
-            n2 = state.pop(("n2", q))
-            dt = state.pop(("dt", q))
-            rn = small.tile([P, V, QUAD], I32)
-            nw = small.tile([P, V, QUAD], F32)
-            sc = small.tile([P, len(PAIRS), QUAD], F32)
-            zz = small.tile([P, len(PAIRS), QUAD], F32)
-            nc.vector.tensor_scalar(out=rn[:], in0=n2[:].bitcast(I32), scalar1=-0.5, scalar2=RSQRT_BITS,
-                                    op0=ALU.mult, op1=ALU.add)
+        def take_small():
+            if pending:
+                pending.pop(0)()
+
+        dot_queue = [(t, n) for t in range(NT) for n in range(len(PAIRS))]
+
+        def next_dot():
+            t, n = dot_queue.pop(0)
+            o, k = t // OCT, t % OCT
+            if k == 0 and n == 0:
+                dt = small.tile([P, len(PAIRS), OCT], F32)
+                state[("dt", o)] = dt
+            dt = state[("dt", o)]
+            i, j = PAIRS[n]
+            q, r = t // QUAD, t % QUAD
+            jv = junk.tile([P, D], BF16)
+            nc.vector.scalar_tensor_tensor(
+                out=jv[:], in0=xt[(i, q)][:, r, :], scalar=1.0, in1=xt[(j, q)][:, r, :],
+                op0=ALU.mult, op1=ALU.mult, accum_out=dt[:, n, k:k + 1],
+            )
+            take_small()
+
+        def scales_of(o):
+            n2 = state.pop(("n2", o))
+            rn = small.tile([P, V, OCT], I32)
+            nw = small.tile([P, V, OCT], F32)
+            sc = small.tile([P, len(PAIRS), OCT], F32)
             y = rn[:].bitcast(F32)
-            for step in range(NEWTON_STEPS):
-                nc.gpsimd.tensor_tensor(out=nw[:], in0=n2[:], in1=y, op=ALU.mult)
-                nc.gpsimd.tensor_tensor(out=nw[:], in0=nw[:], in1=y, op=ALU.mult)
-                nc.gpsimd.tensor_scalar(out=nw[:], in0=nw[:], scalar1=-0.5, scalar2=1.5,
-                                        op0=ALU.mult, op1=ALU.add)
-                nc.gpsimd.tensor_tensor(out=y, in0=nw[:], in1=y, op=ALU.mult)
-            nc.gpsimd.tensor_tensor(out=sc[:, 0:3, :], in0=y[:, 0:1, :].to_broadcast([P, 3, QUAD]),
-                                    in1=y[:, 1:4, :], op=ALU.mult)
-            nc.gpsimd.tensor_tensor(out=sc[:, 3, :], in0=y[:, 1, :], in1=y[:, 2, :], op=ALU.mult)
-            nc.gpsimd.tensor_tensor(out=zz[:], in0=dt[:], in1=sc[:], op=ALU.mult)
-            state[("s", q)] = sc
-            state[("z", q)] = zz
 
-        def first_column(q):
-            if q % 2 == 0:
-                ot = opool.tile([P, NCOMBO, OCT, ROW], F32)
-                state[("o", q // 2)] = ot
-            ot = state[("o", q // 2)]
-            zz = state.pop(("z", q))
-            r = QUAD * (q % 2)
-            nc.scalar.activation(out=ot[:, 0:3, r:r + QUAD, 0], in_=zz[:, 0:3, :], func=ACT.Exp)
-            nc.scalar.activation(out=ot[:, 3:8:2, r:r + QUAD, 0], in_=zz[:, 0:3, :], func=ACT.Exp)
-            nc.scalar.activation(out=ot[:, 4:7:2, r:r + QUAD, 0],
-                                 in_=zz[:, 3:4, :].to_broadcast([P, 2, QUAD]), func=ACT.Exp)
+            def guess():
+                nc.vector.tensor_scalar(out=rn[:], in0=n2[:].bitcast(I32), scalar1=-0.5, scalar2=RSQRT_BITS,
+                                        op0=ALU.mult, op1=ALU.add)
+
+            def newton_a():
+                nc.vector.tensor_tensor(out=nw[:], in0=n2[:], in1=y, op=ALU.mult)
+
+            def newton_b():
+                nc.vector.scalar_tensor_tensor(out=nw[:], in0=nw[:], scalar=-0.5, in1=y,
+                                               op0=ALU.mult, op1=ALU.mult)
+
+            def newton_c():
+                nc.vector.scalar_tensor_tensor(out=y, in0=nw[:], scalar=1.5, in1=y,
+                                               op0=ALU.add, op1=ALU.mult)
+
+            def scale_a():
+                nc.vector.tensor_tensor(out=sc[:, 0:3, :], in0=y[:, 0:1, :].to_broadcast([P, 3, OCT]),
+                                        in1=y[:, 1:4, :], op=ALU.mult)
+
+            def scale_b():
+                nc.vector.tensor_tensor(out=sc[:, 3, :], in0=y[:, 1, :], in1=y[:, 2, :], op=ALU.mult)
+
+            pending.append(guess)
+            pending.extend([newton_a, newton_b, newton_c] * NEWTON_STEPS)
+            pending.extend([scale_a, scale_b])
+            state[("s", o)] = sc
+
+        def cosines(o):
+            zz = small.tile([P, len(PAIRS), OCT], F32)
+            nc.vector.tensor_tensor(out=zz[:], in0=state.pop(("dt", o))[:], in1=state[("s", o)][:], op=ALU.mult)
+            state[("z", o)] = zz
+
+        def first_column(o):
+            zz = state.pop(("z", o))
+            ot = state[("o", o)]
+            nc.scalar.activation(out=ot[:, 0:3, :, 0], in_=zz[:, 0:3, :], func=ACT.Exp)
+            nc.scalar.activation(out=ot[:, 3:8:2, :, 0], in_=zz[:, 0:3, :], func=ACT.Exp)
+            nc.scalar.activation(out=ot[:, 4:7:2, :, 0],
+                                 in_=zz[:, 3:4, :].to_broadcast([P, 2, OCT]), func=ACT.Exp)
 
         def store(o, lo, hi):
             ot = state[("o", o)]
@@ -231,20 +260,21 @@ def tile_memorymoco_pa_t_kernel(tc, x0, x1, x2, x3, mem0, mem1, mem2, mem3, out)
 
         for t in range(LEAD):
             squares(t)
-            dots(t)
+            for n in range(len(PAIRS)):
+                next_dot()
             if t == 1:
                 copy_out("mem")
             if t == 2:
                 quantise("mem", mem_codes, mem_scales)
-            if t % QUAD == QUAD - 1:
-                scales_of(t // QUAD)
+            if t % OCT == OCT - 1:
+                scales_of(t // OCT)
 
         cuts = {}
         for o in range(NT // OCT):
-            cuts[OCT * o + 3] = (o, 0, 512)
-            cuts[OCT * o + 7] = (o, 512, OCT * ROW)
+            cuts[OCT * o + 4] = (o, 0, 640)
+            cuts[OCT * o + 7] = (o, 640, OCT * ROW)
         last = NT // OCT - 1
-        cuts[OCT * last + 5] = (last, 512, 768)
+        cuts[OCT * last + 5] = (last, 640, 768)
         cuts[OCT * last + 6] = (last, 768, 896)
         cuts[OCT * last + 7] = (last, 896, OCT * ROW)
 
@@ -258,15 +288,19 @@ def tile_memorymoco_pa_t_kernel(tc, x0, x1, x2, x3, mem0, mem1, mem2, mem3, out)
                 products(i - 1)
             if 0 <= i - 2 < NT:
                 t = i - 2
-                if t % QUAD == 0:
-                    first_column(t // QUAD)
+                if t % OCT == QUAD:
+                    first_column(t // OCT)
                 exps(t)
                 if t in cuts:
                     o, lo, hi = cuts[t]
                     store(o, lo, hi)
-            if i >= 0 and i + LEAD < NT:
-                t = i + LEAD
-                squares(t)
-                dots(t)
-                if t % QUAD == QUAD - 1:
-                    scales_of(t // QUAD)
+            if i >= 0:
+                if i + LEAD < NT:
+                    squares(i + LEAD)
+                for n in range(DOTS_PER_STEP):
+                    if dot_queue:
+                        next_dot()
+                if i + LEAD < NT and (i + LEAD) % OCT == OCT - 1:
+                    scales_of((i + LEAD) // OCT)
+                if i % OCT == QUAD + 1 and i - 1 < NT:
+                    cosines(i // OCT)

@@ -21,14 +21,22 @@ NCOMBO = 8
 ROW = Q + 1
 QUAD = 4
 OCT = 8
-LEAD = 10
-DOTS_PER_STEP = 3
-SCALAR_COPY_FROM = NT - LEAD
 PAIRS = ((0, 1), (0, 2), (0, 3), (1, 2))
 RSQRT_BITS = float(0x5F3759DF)
 NEWTON_STEPS = 3
 
+LEAD = 10
+BATCHES = ((0, 8), (8, 16), (16, 24), (24, 28), (28, 32))
+BATCH_OF = [b for b, (lo, hi) in enumerate(BATCHES) for t in range(lo, hi)]
+SQUARES_END = 25
+DOTS_END = NT - 2
+GRAM_STEPS = 25
+
 FLOPS = 2 * NCOMBO * B * ROW * D
+
+
+def share(left, steps):
+    return -(-left // steps) if steps > 0 else left
 
 
 def tile_memorymoco_pa_t_kernel(tc, x0, x1, x2, x3, mem0, mem1, mem2, mem3, out):
@@ -78,37 +86,56 @@ def tile_memorymoco_pa_t_kernel(tc, x0, x1, x2, x3, mem0, mem1, mem2, mem3, out)
 
         state = {}
 
-        def rows_of(v, t):
-            return xt[(v, t // QUAD)][:].bitcast(F32)[:, t % QUAD, :]
+        pending = []
+
+        def take_small():
+            if pending:
+                pending.pop(0)()
+
+        def row_of(v, t):
+            return xt[(v, t // QUAD)][:, t % QUAD, :]
 
         def transposes(key, sources):
-            banks = []
             tpa = psum.tile([P, 2, 2, P], F32)
             tpb = psum.tile([P, 2, 2, P], F32)
-            for n in range(V):
-                bank = tpa if n < 2 else tpb
+            for v in range(V):
+                bank = tpa if v < 2 else tpb
                 for u in range(2):
-                    nc.tensor.transpose(bank[:, n % 2, u, :], sources[n][:, u:2 * P:2], ident[:])
-            banks.append(tpa)
-            banks.append(tpb)
-            state[("tp", key)] = banks
+                    nc.tensor.transpose(bank[:, v % 2, u, :], sources[v][:, u:2 * P:2], ident[:])
+            state[("tp", key)] = (tpa, tpb)
 
-        def copy_out(key):
-            banks = state.pop(("tp", key))
+        def copy_out(key, on_scalar):
+            banks = state[("tp", key)]
             gt = work.tile([P, V, P, 4], BF16, align_bytes=64)
             gtw = gt[:].bitcast(F32)
             for h in range(2):
                 dst = gtw[:, 2 * h:2 * h + 2, :, :]
                 src = banks[h][:].rearrange("w n u p -> w n p u")
-                if key != "mem" and key >= SCALAR_COPY_FROM:
+                if on_scalar:
                     nc.scalar.copy(out=dst, in_=src)
                 else:
                     nc.vector.tensor_copy(out=dst, in_=src)
                     take_small()
             state[("gt", key)] = gt
 
+        def gram(t):
+            gt = state[("gt", t)]
+            dst = state[("tp", t)][0][:, 0, 0, :]
+            for j in range(4):
+                nc.tensor.matmul(dst, lhsT=gt[:, 0, :, j], rhs=gt[:, 1, :, j], start=(j == 0), stop=(j == 3))
+
+        def diagonal(t):
+            bank = state[("tp", t)][0]
+            jd = junk.tile([P, P], BF16)
+            lo, dt = dot_tile(t)
+            nc.vector.scalar_tensor_tensor(
+                out=jd[:], in0=bank[:, 0, 0, :], scalar=1.0, in1=ident[:],
+                op0=ALU.mult, op1=ALU.mult, accum_out=dt[:, 0, t - lo:t - lo + 1],
+            )
+            take_small()
+
         def quantise(key, codes, scales):
-            gt = state.pop(("gt", key))
+            gt = state[("gt", key)]
             nc.vector.quantize_mx(
                 out=codes[:].bitcast(FP8X4),
                 scales=scales[:],
@@ -134,7 +161,7 @@ def tile_memorymoco_pa_t_kernel(tc, x0, x1, x2, x3, mem0, mem1, mem2, mem3, out)
             )
 
         def products(t):
-            codes, scales = state.pop(("cd", t))
+            codes, scales = state[("cd", t)]
             ma = psum.tile([P, 4, Q], F32)
             mb = psum.tile([P, 4, Q], F32)
             maf = ma[:].rearrange("p n q -> p (n q)")
@@ -148,14 +175,15 @@ def tile_memorymoco_pa_t_kernel(tc, x0, x1, x2, x3, mem0, mem1, mem2, mem3, out)
             state[("mm", t)] = (ma, mb)
 
         def exps(t):
-            ma, mb = state.pop(("mm", t))
-            if t % OCT == 0:
+            ma, mb = state[("mm", t)]
+            b = BATCH_OF[t]
+            k = t - BATCHES[b][0]
+            sc = state[("s", b)]
+            r = t % OCT
+            if r == 0:
                 ot = opool.tile([P, NCOMBO, OCT, ROW], F32)
                 state[("o", t // OCT)] = ot
             ot = state[("o", t // OCT)]
-            sc = state[("s", t // OCT)]
-            r = t % OCT
-            k = r
             nc.scalar.activation(out=ot[:, 1:6:4, r, 1:ROW], in_=ma[:, 1:4:2, :], func=ACT.Exp,
                                  scale=sc[:, 1, k:k + 1])
             nc.scalar.activation(out=ot[:, 0:4:3, r, 1:ROW], in_=ma[:, 0:3:2, :], func=ACT.Exp,
@@ -165,87 +193,90 @@ def tile_memorymoco_pa_t_kernel(tc, x0, x1, x2, x3, mem0, mem1, mem2, mem3, out)
             nc.scalar.activation(out=ot[:, 4:7:2, r, 1:ROW], in_=mb[:, 2:4, :], func=ACT.Exp,
                                  scale=sc[:, 3, k:k + 1])
 
-        def squares(t):
-            o, k = t // OCT, t % OCT
-            if k == 0:
+        square_queue = [(t, v) for t in range(NT) for v in range(V)]
+        dot_queue = [(t, n) for t in range(NT) for n in range(len(PAIRS)) if n > 0 or t >= GRAM_STEPS]
+
+        def next_square():
+            t, v = square_queue.pop(0)
+            b = BATCH_OF[t]
+            k = t - BATCHES[b][0]
+            if ("n2", b) not in state:
                 n2 = small.tile([P, V, OCT], F32)
-                state[("n2", o)] = n2
-            n2 = state[("n2", o)]
-            for v in range(V):
-                js = junk.tile([P, D], BF16)
-                nc.scalar.activation(out=js[:], in_=xt[(v, t // QUAD)][:, t % QUAD, :], func=ACT.Square,
-                                     scale=sqrt_temp, accum_out=n2[:, v, k:k + 1])
+                state[("n2", b)] = n2
+            js = junk.tile([P, D], BF16)
+            nc.scalar.activation(out=js[:], in_=row_of(v, t), func=ACT.Square,
+                                 scale=sqrt_temp, accum_out=state[("n2", b)][:, v, k:k + 1])
 
-        pending = []
-
-        def take_small():
-            if pending:
-                pending.pop(0)()
-
-        dot_queue = [(t, n) for t in range(NT) for n in range(len(PAIRS))]
+        def dot_tile(t):
+            b = BATCH_OF[t]
+            if ("dt", b) not in state:
+                dt = small.tile([P, len(PAIRS), OCT], F32)
+                state[("dt", b)] = dt
+            return BATCHES[b][0], state[("dt", b)]
 
         def next_dot():
             t, n = dot_queue.pop(0)
-            o, k = t // OCT, t % OCT
-            if k == 0 and n == 0:
-                dt = small.tile([P, len(PAIRS), OCT], F32)
-                state[("dt", o)] = dt
-            dt = state[("dt", o)]
+            lo, dt = dot_tile(t)
             i, j = PAIRS[n]
-            q, r = t // QUAD, t % QUAD
             jv = junk.tile([P, D], BF16)
             nc.vector.scalar_tensor_tensor(
-                out=jv[:], in0=xt[(i, q)][:, r, :], scalar=1.0, in1=xt[(j, q)][:, r, :],
-                op0=ALU.mult, op1=ALU.mult, accum_out=dt[:, n, k:k + 1],
+                out=jv[:], in0=row_of(i, t), scalar=1.0, in1=row_of(j, t),
+                op0=ALU.mult, op1=ALU.mult, accum_out=dt[:, n, t - lo:t - lo + 1],
             )
             take_small()
 
-        def scales_of(o):
-            n2 = state.pop(("n2", o))
+        def scales_of(b):
+            w = BATCHES[b][1] - BATCHES[b][0]
+            n2 = state[("n2", b)][:, :, 0:w]
             rn = small.tile([P, V, OCT], I32)
-            nw = small.tile([P, V, OCT], F32)
-            sc = small.tile([P, len(PAIRS), OCT], F32)
-            y = rn[:].bitcast(F32)
+            nwt = small.tile([P, V, OCT], F32)
+            sct = small.tile([P, len(PAIRS), OCT], F32)
+            bits = rn[:, :, 0:w]
+            y = rn[:].bitcast(F32)[:, :, 0:w]
+            nw = nwt[:, :, 0:w]
 
             def guess():
-                nc.vector.tensor_scalar(out=rn[:], in0=n2[:].bitcast(I32), scalar1=-0.5, scalar2=RSQRT_BITS,
-                                        op0=ALU.mult, op1=ALU.add)
+                nc.vector.tensor_scalar(out=bits, in0=state[("n2", b)][:].bitcast(I32)[:, :, 0:w], scalar1=-0.5,
+                                        scalar2=RSQRT_BITS, op0=ALU.mult, op1=ALU.add)
 
             def newton_a():
-                nc.vector.tensor_tensor(out=nw[:], in0=n2[:], in1=y, op=ALU.mult)
+                nc.vector.tensor_tensor(out=nw, in0=n2, in1=y, op=ALU.mult)
 
             def newton_b():
-                nc.vector.scalar_tensor_tensor(out=nw[:], in0=nw[:], scalar=-0.5, in1=y,
-                                               op0=ALU.mult, op1=ALU.mult)
+                nc.vector.scalar_tensor_tensor(out=nw, in0=nw, scalar=-0.5, in1=y, op0=ALU.mult, op1=ALU.mult)
 
             def newton_c():
-                nc.vector.scalar_tensor_tensor(out=y, in0=nw[:], scalar=1.5, in1=y,
-                                               op0=ALU.add, op1=ALU.mult)
+                nc.vector.scalar_tensor_tensor(out=y, in0=nw, scalar=1.5, in1=y, op0=ALU.add, op1=ALU.mult)
 
             def scale_a():
-                nc.vector.tensor_tensor(out=sc[:, 0:3, :], in0=y[:, 0:1, :].to_broadcast([P, 3, OCT]),
+                nc.vector.tensor_tensor(out=sct[:, 0:3, 0:w], in0=y[:, 0:1, :].to_broadcast([P, 3, w]),
                                         in1=y[:, 1:4, :], op=ALU.mult)
 
             def scale_b():
-                nc.vector.tensor_tensor(out=sc[:, 3, :], in0=y[:, 1, :], in1=y[:, 2, :], op=ALU.mult)
+                nc.vector.tensor_tensor(out=sct[:, 3, 0:w], in0=y[:, 1, :], in1=y[:, 2, :], op=ALU.mult)
+                state[("s", b)] = sct
 
             pending.append(guess)
             pending.extend([newton_a, newton_b, newton_c] * NEWTON_STEPS)
             pending.extend([scale_a, scale_b])
-            state[("s", o)] = sc
 
-        def cosines(o):
+        def cosines(b):
+            w = BATCHES[b][1] - BATCHES[b][0]
             zz = small.tile([P, len(PAIRS), OCT], F32)
-            nc.vector.tensor_tensor(out=zz[:], in0=state.pop(("dt", o))[:], in1=state[("s", o)][:], op=ALU.mult)
-            state[("z", o)] = zz
+            nc.vector.tensor_tensor(out=zz[:, :, 0:w], in0=state[("dt", b)][:, :, 0:w],
+                                    in1=state[("s", b)][:, :, 0:w], op=ALU.mult)
+            state[("z", b)] = zz
 
-        def first_column(o):
-            zz = state.pop(("z", o))
-            ot = state[("o", o)]
-            nc.scalar.activation(out=ot[:, 0:3, :, 0], in_=zz[:, 0:3, :], func=ACT.Exp)
-            nc.scalar.activation(out=ot[:, 3:8:2, :, 0], in_=zz[:, 0:3, :], func=ACT.Exp)
-            nc.scalar.activation(out=ot[:, 4:7:2, :, 0],
-                                 in_=zz[:, 3:4, :].to_broadcast([P, 2, OCT]), func=ACT.Exp)
+        def first_column(b):
+            lo, hi = BATCHES[b]
+            w = hi - lo
+            zz = state[("z", b)]
+            ot = state[("o", lo // OCT)]
+            r = lo % OCT
+            nc.scalar.activation(out=ot[:, 0:3, r:r + w, 0], in_=zz[:, 0:3, 0:w], func=ACT.Exp)
+            nc.scalar.activation(out=ot[:, 3:8:2, r:r + w, 0], in_=zz[:, 0:3, 0:w], func=ACT.Exp)
+            nc.scalar.activation(out=ot[:, 4:7:2, r:r + w, 0],
+                                 in_=zz[:, 3:4, 0:w].to_broadcast([P, 2, w]), func=ACT.Exp)
 
         def store(o, lo, hi):
             ot = state[("o", o)]
@@ -257,50 +288,58 @@ def tile_memorymoco_pa_t_kernel(tc, x0, x1, x2, x3, mem0, mem1, mem2, mem3, out)
 
         mem_words = mem_nat[:].bitcast(F32)
         transposes("mem", [mem_words[:, j, :] for j in range(V)])
-
         for t in range(LEAD):
-            squares(t)
+            for v in range(V):
+                next_square()
             for n in range(len(PAIRS)):
                 next_dot()
             if t == 1:
-                copy_out("mem")
+                copy_out("mem", False)
             if t == 2:
                 quantise("mem", mem_codes, mem_scales)
-            if t % OCT == OCT - 1:
-                scales_of(t // OCT)
+            if t == OCT:
+                scales_of(0)
 
         cuts = {}
-        for o in range(NT // OCT):
-            cuts[OCT * o + 4] = (o, 0, 640)
-            cuts[OCT * o + 7] = (o, 640, OCT * ROW)
         last = NT // OCT - 1
-        cuts[OCT * last + 5] = (last, 640, 768)
+        for o in range(last):
+            cuts[OCT * o + 7] = (o, 0, OCT * ROW)
+        cuts[OCT * last + 3] = (last, 0, 512)
+        cuts[OCT * last + 5] = (last, 512, 768)
         cuts[OCT * last + 6] = (last, 768, 896)
         cuts[OCT * last + 7] = (last, 896, OCT * ROW)
 
+        cosine_step = {}
+        for b, (lo, hi) in enumerate(BATCHES):
+            cosine_step[min(hi, DOTS_END)] = b
+        batches_due = list(range(1, len(BATCHES)))
+
         for i in range(-1, NT + 2):
-            if 0 <= i + 1 < NT:
-                transposes(i + 1, [rows_of(v, i + 1) for v in range(V)])
+            if i + 1 < NT:
+                transposes(i + 1, [row_of(v, i + 1).bitcast(F32) for v in range(V)])
             if 0 <= i < NT:
-                copy_out(i)
+                copy_out(i, i >= SQUARES_END)
+                if i < GRAM_STEPS:
+                    gram(i)
             if 0 <= i - 1 < NT:
                 quantise_step(i - 1)
                 products(i - 1)
+            if i in cosine_step:
+                cosines(cosine_step[i])
+            if i - 1 in cosine_step:
+                first_column(cosine_step[i - 1])
             if 0 <= i - 2 < NT:
-                t = i - 2
-                if t % OCT == QUAD:
-                    first_column(t // OCT)
-                exps(t)
-                if t in cuts:
-                    o, lo, hi = cuts[t]
+                exps(i - 2)
+                if i - 2 in cuts:
+                    o, lo, hi = cuts[i - 2]
                     store(o, lo, hi)
             if i >= 0:
-                if i + LEAD < NT:
-                    squares(i + LEAD)
-                for n in range(DOTS_PER_STEP):
-                    if dot_queue:
-                        next_dot()
-                if i + LEAD < NT and (i + LEAD) % OCT == OCT - 1:
-                    scales_of((i + LEAD) // OCT)
-                if i % OCT == QUAD + 1 and i - 1 < NT:
-                    cosines(i // OCT)
+                squares_before = len(square_queue)
+                for n in range(share(len(square_queue), SQUARES_END - i)):
+                    next_square()
+                for n in range(share(len(dot_queue), DOTS_END - i)):
+                    next_dot()
+                if i < GRAM_STEPS:
+                    diagonal(i)
+                if batches_due and V * (NT - BATCHES[batches_due[0]][1]) >= squares_before:
+                    scales_of(batches_due.pop(0))

@@ -25,11 +25,14 @@ PAIRS = ((0, 1), (0, 2), (0, 3), (1, 2))
 RSQRT_BITS = float(0x5F3759DF)
 NEWTON_STEPS = 3
 
-LEAD = 10
-BATCHES = ((0, 8), (8, 16), (16, 24), (24, 28), (28, 32))
-BATCH_OF = [b for b, (lo, hi) in enumerate(BATCHES) for t in range(lo, hi)]
-SQUARES_END = 25
-DOTS_END = NT - 2
+LEAD = 9
+COLUMNS = ((0, 8), (8, 16), (16, 20), (20, 24), (24, 28), (28, 32))
+STORES = ((0, 8), (8, 16), (16, 20), (20, 24), (24, 26), (26, 28), (28, 30), (30, 31), (31, 32))
+SQUARES_END = 21
+DOTS_AHEAD = 26
+SCALAR_FIRST = range(23, 28)
+SCALAR_SECOND = range(22, 28)
+DOTS_END = 30
 GRAM_STEPS = 25
 
 FLOPS = 2 * NCOMBO * B * ROW * D
@@ -55,22 +58,18 @@ def tile_memorymoco_pa_t_kernel(tc, x0, x1, x2, x3, mem0, mem1, mem2, mem3, out)
         ctx.enter_context(tc.manual_schedule())
 
         mem_nat = keep.tile([P, V, D], BF16, name="mem_nat")
-        for j in range(V):
-            nc.scalar.dma_start(out=mem_nat[:, j, :], in_=mems[j])
         xt = {}
-        for q in range(NT // QUAD):
-            for v in range(V):
+        for v in range(V):
+            for q in range(NT // QUAD):
                 xq = keep.tile([P, QUAD, D], BF16, name="x%d_%d" % (v, q))
-                src = xs[v].rearrange("(p t) d -> p t d", t=NT)
                 xt[(v, q)] = xq
-                if q > 0:
-                    nc.sync.dma_start(out=xq[:], in_=src[:, QUAD * q:QUAD * q + QUAD, :])
-            if q == 0:
-                for half in range(2):
-                    for v in range(V):
-                        src = xs[v].rearrange("(p t) d -> p t d", t=NT)
-                        nc.sync.dma_start(out=xt[(v, 0)][:, 2 * half:2 * half + 2, :],
-                                          in_=src[:, 2 * half:2 * half + 2, :])
+        for lo, hi in ((0, 1), (1, 2), (2, 4)) + tuple((t, t + QUAD) for t in range(QUAD, NT, QUAD)):
+            for v in range(V):
+                src = xs[v].rearrange("(p t) d -> p t d", t=NT)
+                nc.sync.dma_start(out=xt[(v, lo // QUAD)][:, lo % QUAD:lo % QUAD + hi - lo, :], in_=src[:, lo:hi, :])
+            if lo == 1:
+                for j in range(V):
+                    nc.sync.dma_start(out=mem_nat[:, j, :], in_=mems[j])
 
         ident = keep.tile([P, P], F32, name="ident")
         make_identity(nc, ident[:])
@@ -111,7 +110,7 @@ def tile_memorymoco_pa_t_kernel(tc, x0, x1, x2, x3, mem0, mem1, mem2, mem3, out)
             for h in range(2):
                 dst = gtw[:, 2 * h:2 * h + 2, :, :]
                 src = banks[h][:].rearrange("w n u p -> w n p u")
-                if on_scalar:
+                if on_scalar[h]:
                     nc.scalar.copy(out=dst, in_=src)
                 else:
                     nc.vector.tensor_copy(out=dst, in_=src)
@@ -127,10 +126,11 @@ def tile_memorymoco_pa_t_kernel(tc, x0, x1, x2, x3, mem0, mem1, mem2, mem3, out)
         def diagonal(t):
             bank = state[("tp", t)][0]
             jd = junk.tile([P, P], BF16)
-            lo, dt = dot_tile(t)
+            dt = dot_tile(t)
+            k = t % OCT
             nc.vector.scalar_tensor_tensor(
                 out=jd[:], in0=bank[:, 0, 0, :], scalar=1.0, in1=ident[:],
-                op0=ALU.mult, op1=ALU.mult, accum_out=dt[:, 0, t - lo:t - lo + 1],
+                op0=ALU.mult, op1=ALU.mult, accum_out=dt[:, 0, k:k + 1],
             )
             take_small()
 
@@ -176,10 +176,8 @@ def tile_memorymoco_pa_t_kernel(tc, x0, x1, x2, x3, mem0, mem1, mem2, mem3, out)
 
         def exps(t):
             ma, mb = state[("mm", t)]
-            b = BATCH_OF[t]
-            k = t - BATCHES[b][0]
-            sc = state[("s", b)]
-            r = t % OCT
+            sc = state[("s", t // OCT)]
+            r = k = t % OCT
             if r == 0:
                 ot = opool.tile([P, NCOMBO, OCT, ROW], F32)
                 state[("o", t // OCT)] = ot
@@ -198,8 +196,7 @@ def tile_memorymoco_pa_t_kernel(tc, x0, x1, x2, x3, mem0, mem1, mem2, mem3, out)
 
         def next_square():
             t, v = square_queue.pop(0)
-            b = BATCH_OF[t]
-            k = t - BATCHES[b][0]
+            b, k = t // OCT, t % OCT
             if ("n2", b) not in state:
                 n2 = small.tile([P, V, OCT], F32)
                 state[("n2", b)] = n2
@@ -208,117 +205,111 @@ def tile_memorymoco_pa_t_kernel(tc, x0, x1, x2, x3, mem0, mem1, mem2, mem3, out)
                                  scale=sqrt_temp, accum_out=state[("n2", b)][:, v, k:k + 1])
 
         def dot_tile(t):
-            b = BATCH_OF[t]
+            b = t // OCT
             if ("dt", b) not in state:
                 dt = small.tile([P, len(PAIRS), OCT], F32)
                 state[("dt", b)] = dt
-            return BATCHES[b][0], state[("dt", b)]
+            return state[("dt", b)]
 
         def next_dot():
             t, n = dot_queue.pop(0)
-            lo, dt = dot_tile(t)
+            dt = dot_tile(t)
+            k = t % OCT
             i, j = PAIRS[n]
             jv = junk.tile([P, D], BF16)
             nc.vector.scalar_tensor_tensor(
                 out=jv[:], in0=row_of(i, t), scalar=1.0, in1=row_of(j, t),
-                op0=ALU.mult, op1=ALU.mult, accum_out=dt[:, n, t - lo:t - lo + 1],
+                op0=ALU.mult, op1=ALU.mult, accum_out=dt[:, n, k:k + 1],
             )
             take_small()
 
         def scales_of(b):
-            w = BATCHES[b][1] - BATCHES[b][0]
-            n2 = state[("n2", b)][:, :, 0:w]
+            n2 = state[("n2", b)]
             rn = small.tile([P, V, OCT], I32)
-            nwt = small.tile([P, V, OCT], F32)
-            sct = small.tile([P, len(PAIRS), OCT], F32)
-            bits = rn[:, :, 0:w]
-            y = rn[:].bitcast(F32)[:, :, 0:w]
-            nw = nwt[:, :, 0:w]
+            nw = small.tile([P, V, OCT], F32)
+            sc = small.tile([P, len(PAIRS), OCT], F32)
+            y = rn[:].bitcast(F32)
 
             def guess():
-                nc.vector.tensor_scalar(out=bits, in0=state[("n2", b)][:].bitcast(I32)[:, :, 0:w], scalar1=-0.5,
-                                        scalar2=RSQRT_BITS, op0=ALU.mult, op1=ALU.add)
+                nc.vector.tensor_scalar(out=rn[:], in0=n2[:].bitcast(I32), scalar1=-0.5, scalar2=RSQRT_BITS,
+                                        op0=ALU.mult, op1=ALU.add)
 
             def newton_a():
-                nc.vector.tensor_tensor(out=nw, in0=n2, in1=y, op=ALU.mult)
+                nc.vector.tensor_tensor(out=nw[:], in0=n2[:], in1=y, op=ALU.mult)
 
             def newton_b():
-                nc.vector.scalar_tensor_tensor(out=nw, in0=nw, scalar=-0.5, in1=y, op0=ALU.mult, op1=ALU.mult)
+                nc.vector.scalar_tensor_tensor(out=nw[:], in0=nw[:], scalar=-0.5, in1=y,
+                                               op0=ALU.mult, op1=ALU.mult)
 
             def newton_c():
-                nc.vector.scalar_tensor_tensor(out=y, in0=nw, scalar=1.5, in1=y, op0=ALU.add, op1=ALU.mult)
+                nc.vector.scalar_tensor_tensor(out=y, in0=nw[:], scalar=1.5, in1=y,
+                                               op0=ALU.add, op1=ALU.mult)
 
             def scale_a():
-                nc.vector.tensor_tensor(out=sct[:, 0:3, 0:w], in0=y[:, 0:1, :].to_broadcast([P, 3, w]),
+                nc.vector.tensor_tensor(out=sc[:, 0:3, :], in0=y[:, 0:1, :].to_broadcast([P, 3, OCT]),
                                         in1=y[:, 1:4, :], op=ALU.mult)
 
             def scale_b():
-                nc.vector.tensor_tensor(out=sct[:, 3, 0:w], in0=y[:, 1, :], in1=y[:, 2, :], op=ALU.mult)
-                state[("s", b)] = sct
+                nc.vector.tensor_tensor(out=sc[:, 3, :], in0=y[:, 1, :], in1=y[:, 2, :], op=ALU.mult)
+                state[("s", b)] = sc
 
             pending.append(guess)
             pending.extend([newton_a, newton_b, newton_c] * NEWTON_STEPS)
             pending.extend([scale_a, scale_b])
 
-        def cosines(b):
-            w = BATCHES[b][1] - BATCHES[b][0]
+        def cosines(c):
+            lo, hi = COLUMNS[c]
+            b, r, w = lo // OCT, lo % OCT, hi - lo
             zz = small.tile([P, len(PAIRS), OCT], F32)
-            nc.vector.tensor_tensor(out=zz[:, :, 0:w], in0=state[("dt", b)][:, :, 0:w],
-                                    in1=state[("s", b)][:, :, 0:w], op=ALU.mult)
-            state[("z", b)] = zz
+            nc.vector.tensor_tensor(out=zz[:, :, 0:w], in0=state[("dt", b)][:, :, r:r + w],
+                                    in1=state[("s", b)][:, :, r:r + w], op=ALU.mult)
+            state[("z", c)] = zz
 
-        def first_column(b):
-            lo, hi = BATCHES[b]
-            w = hi - lo
-            zz = state[("z", b)]
+        def first_column(c):
+            lo, hi = COLUMNS[c]
+            r, w = lo % OCT, hi - lo
+            zz = state[("z", c)]
             ot = state[("o", lo // OCT)]
-            r = lo % OCT
             nc.scalar.activation(out=ot[:, 0:3, r:r + w, 0], in_=zz[:, 0:3, 0:w], func=ACT.Exp)
             nc.scalar.activation(out=ot[:, 3:8:2, r:r + w, 0], in_=zz[:, 0:3, 0:w], func=ACT.Exp)
             nc.scalar.activation(out=ot[:, 4:7:2, r:r + w, 0],
                                  in_=zz[:, 3:4, 0:w].to_broadcast([P, 2, w]), func=ACT.Exp)
 
-        def store(o, lo, hi):
+        def store(lo, hi):
+            o = lo // OCT
             ot = state[("o", o)]
-            base = o * OCT * ROW
+            first = Q * (lo - o * OCT)
+            end = OCT * ROW if hi == (o + 1) * OCT else Q * (hi - o * OCT)
             nc.sync.dma_start(
-                out=out_view[:, :, base + lo:base + hi],
-                in_=ot[:].rearrange("p c t q -> p c (t q)")[:, :, lo:hi],
+                out=out_view[:, :, o * OCT * ROW + first:o * OCT * ROW + end],
+                in_=ot[:].rearrange("p c t q -> p c (t q)")[:, :, first:end],
             )
 
         mem_words = mem_nat[:].bitcast(F32)
         transposes("mem", [mem_words[:, j, :] for j in range(V)])
+        dots_left = len(dot_queue) - DOTS_AHEAD
         for t in range(LEAD):
             for v in range(V):
                 next_square()
-            for n in range(len(PAIRS)):
+            for n in range(share(len(dot_queue) - dots_left, LEAD - t)):
                 next_dot()
             if t == 1:
-                copy_out("mem", False)
+                copy_out("mem", (False, False))
             if t == 2:
                 quantise("mem", mem_codes, mem_scales)
             if t == OCT:
                 scales_of(0)
 
-        cuts = {}
-        last = NT // OCT - 1
-        for o in range(last):
-            cuts[OCT * o + 7] = (o, 0, OCT * ROW)
-        cuts[OCT * last + 3] = (last, 0, 512)
-        cuts[OCT * last + 5] = (last, 512, 768)
-        cuts[OCT * last + 6] = (last, 768, 896)
-        cuts[OCT * last + 7] = (last, 896, OCT * ROW)
-
         cosine_step = {}
-        for b, (lo, hi) in enumerate(BATCHES):
-            cosine_step[min(hi, DOTS_END)] = b
-        batches_due = list(range(1, len(BATCHES)))
+        for c, (lo, hi) in enumerate(COLUMNS):
+            cosine_step[max(min(hi, GRAM_STEPS), DOTS_END - (NT - hi))] = c
+        batches_due = list(range(1, NT // OCT))
 
         for i in range(-1, NT + 2):
             if i + 1 < NT:
                 transposes(i + 1, [row_of(v, i + 1).bitcast(F32) for v in range(V)])
             if 0 <= i < NT:
-                copy_out(i, i >= SQUARES_END)
+                copy_out(i, (i in SCALAR_FIRST, i in SCALAR_SECOND))
                 if i < GRAM_STEPS:
                     gram(i)
             if 0 <= i - 1 < NT:
@@ -326,13 +317,13 @@ def tile_memorymoco_pa_t_kernel(tc, x0, x1, x2, x3, mem0, mem1, mem2, mem3, out)
                 products(i - 1)
             if i in cosine_step:
                 cosines(cosine_step[i])
-            if i - 1 in cosine_step:
-                first_column(cosine_step[i - 1])
             if 0 <= i - 2 < NT:
                 exps(i - 2)
-                if i - 2 in cuts:
-                    o, lo, hi = cuts[i - 2]
-                    store(o, lo, hi)
+            if i - 1 in cosine_step:
+                first_column(cosine_step[i - 1])
+            for lo, hi in STORES:
+                if hi == i - 1:
+                    store(lo, hi)
             if i >= 0:
                 squares_before = len(square_queue)
                 for n in range(share(len(square_queue), SQUARES_END - i)):
@@ -341,5 +332,5 @@ def tile_memorymoco_pa_t_kernel(tc, x0, x1, x2, x3, mem0, mem1, mem2, mem3, out)
                     next_dot()
                 if i < GRAM_STEPS:
                     diagonal(i)
-                if batches_due and V * (NT - BATCHES[batches_due[0]][1]) >= squares_before:
+                if batches_due and V * (NT - OCT * (batches_due[0] + 1)) >= squares_before:
                     scales_of(batches_due.pop(0))

@@ -25,14 +25,18 @@ PAIRS = ((0, 1), (0, 2), (0, 3), (1, 2))
 RSQRT_BITS = float(0x5F3759DF)
 NEWTON_STEPS = 3
 
+GROUPS = 4
+GROUP = P // GROUPS
+SHARED_AHEAD = 3
+SHARED_EVERY = 4
 LEAD = 9
 COLUMNS = ((0, 8), (8, 16), (16, 20), (20, 24), (24, 28), (28, 32))
 STORES = ((0, 8), (8, 16), (16, 20), (20, 24), (24, 26), (26, 28), (28, 30), (30, 31), (31, 32))
-SQUARES_END = 21
-DOTS_AHEAD = 26
-SCALAR_FIRST = range(23, 28)
-SCALAR_SECOND = range(22, 28)
-DOTS_END = 30
+SQUARES_END = 22
+DOTS_AHEAD = 7
+SCALAR_FIRST = range(25, 29)
+SCALAR_SECOND = range(31, 31)
+DOTS_END = 28
 GRAM_STEPS = 25
 
 FLOPS = 2 * NCOMBO * B * ROW * D
@@ -54,7 +58,9 @@ def tile_memorymoco_pa_t_kernel(tc, x0, x1, x2, x3, mem0, mem1, mem2, mem3, out)
         work = ctx.enter_context(tc.tile_pool(name="work", bufs=3))
         junk = ctx.enter_context(tc.tile_pool(name="junk", bufs=2))
         small = ctx.enter_context(tc.tile_pool(name="small", bufs=4))
-        psum = ctx.enter_context(tc.psum_pool(name="psum", bufs=2))
+        tp_psum = ctx.enter_context(tc.psum_pool(name="tp_psum", bufs=3))
+        gram_psum = ctx.enter_context(tc.psum_pool(name="gram_psum", bufs=2))
+        mm_psum = ctx.enter_context(tc.psum_pool(name="mm_psum", bufs=3))
         ctx.enter_context(tc.manual_schedule())
 
         mem_nat = keep.tile([P, V, D], BF16, name="mem_nat")
@@ -73,6 +79,14 @@ def tile_memorymoco_pa_t_kernel(tc, x0, x1, x2, x3, mem0, mem1, mem2, mem3, out)
 
         ident = keep.tile([P, P], F32, name="ident")
         make_identity(nc, ident[:])
+        of_view = keep.tile([P, V], F32, name="of_view")
+        nc.vector.tensor_reduce(out=of_view[:], in_=ident[:].rearrange("p (v r) -> p v r", v=V),
+                                axis=mybir.AxisListType.X, op=ALU.add)
+        of_row = keep.tile([P, GROUP], F32, name="of_row")
+        nc.vector.tensor_reduce(out=of_row[:], in_=ident[:].rearrange("p (v r) -> p r v", v=V),
+                                axis=mybir.AxisListType.X, op=ALU.add)
+        on_diag = keep.tile([P, GROUP, GROUPS], F32, name="on_diag")
+        nc.vector.tensor_copy(out=on_diag[:], in_=of_row[:].unsqueeze(2).to_broadcast([P, GROUP, GROUPS]))
         warm_in = keep.tile([P, 1], F32, name="warm_in")
         warm_out = keep.tile([P, 1], F32, name="warm_out")
         nc.vector.memset(warm_in[:], 0.0)
@@ -95,13 +109,14 @@ def tile_memorymoco_pa_t_kernel(tc, x0, x1, x2, x3, mem0, mem1, mem2, mem3, out)
             return xt[(v, t // QUAD)][:, t % QUAD, :]
 
         def transposes(key, sources):
-            tpa = psum.tile([P, 2, 2, P], F32)
-            tpb = psum.tile([P, 2, 2, P], F32)
-            for v in range(V):
-                bank = tpa if v < 2 else tpb
-                for u in range(2):
-                    nc.tensor.transpose(bank[:, v % 2, u, :], sources[v][:, u:2 * P:2], ident[:])
-            state[("tp", key)] = (tpa, tpb)
+            banks = []
+            for h in range(2):
+                tp = tp_psum.tile([P, 2, 2, P], F32)
+                for v in (2 * h, 2 * h + 1):
+                    for u in range(2):
+                        nc.tensor.transpose(tp[:, v % 2, u, :], sources[v][:, u:2 * P:2], ident[:])
+                banks.append(tp)
+            state[("tp", key)] = banks
 
         def copy_out(key, on_scalar):
             banks = state[("tp", key)]
@@ -118,21 +133,29 @@ def tile_memorymoco_pa_t_kernel(tc, x0, x1, x2, x3, mem0, mem1, mem2, mem3, out)
             state[("gt", key)] = gt
 
         def gram(t):
-            gt = state[("gt", t)]
-            dst = state[("tp", t)][0][:, 0, 0, :]
-            for j in range(4):
-                nc.tensor.matmul(dst, lhsT=gt[:, 0, :, j], rhs=gt[:, 1, :, j], start=(j == 0), stop=(j == 3))
+            columns = state[("gt", t)][:].rearrange("w v p j -> w (v p) j")
+            gm = gram_psum.tile([P, GROUPS, P], F32)
+            for g in range(GROUPS):
+                for j in range(4):
+                    nc.tensor.matmul(gm[:, 0, GROUP * g:GROUP * g + GROUP], lhsT=columns[:, g:V * P:GROUPS, j],
+                                     rhs=columns[:, g:P:GROUPS, j], start=(j == 0), stop=(j == 3))
+            state[("gm", t)] = gm
 
-        def diagonal(t):
-            bank = state[("tp", t)][0]
-            jd = junk.tile([P, P], BF16)
-            dt = dot_tile(t)
-            k = t % OCT
-            nc.vector.scalar_tensor_tensor(
-                out=jd[:], in0=bank[:, 0, 0, :], scalar=1.0, in1=ident[:],
-                op0=ALU.mult, op1=ALU.mult, accum_out=dt[:, 0, k:k + 1],
-            )
+        def mask(t):
+            gm = state[("gm", t)]
+            hd = work.tile([P, P], F32)
+            nc.vector.tensor_tensor(
+                out=hd[:].rearrange("p (n g) -> p n g", g=GROUPS),
+                in0=gm[:, 0, :].rearrange("p (g n) -> p n g", g=GROUPS), in1=on_diag[:], op=ALU.mult)
             take_small()
+            state[("hd", t)] = hd
+
+        def regroup(t):
+            nc.tensor.matmul(state[("gm", t)][:, 1, 0:V], lhsT=state[("hd", t)][:], rhs=of_view[:],
+                             start=True, stop=True)
+
+        def gram_dots(t):
+            nc.vector.tensor_copy(out=dot_tile(t)[:, 0:3, t % OCT], in_=state[("gm", t)][:, 1, 1:V])
 
         def quantise(key, codes, scales):
             gt = state[("gt", key)]
@@ -162,20 +185,20 @@ def tile_memorymoco_pa_t_kernel(tc, x0, x1, x2, x3, mem0, mem1, mem2, mem3, out)
 
         def products(t):
             codes, scales = state[("cd", t)]
-            ma = psum.tile([P, 4, Q], F32)
-            mb = psum.tile([P, 4, Q], F32)
-            maf = ma[:].rearrange("p n q -> p (n q)")
-            mx_pass(maf[:, 0:2 * Q], codes, scales, 0, 1, 3)
-            mx_pass(ma[:, 2, :], codes, scales, 1, 0, 1)
-            mx_pass(ma[:, 3, :], codes, scales, 2, 0, 1)
-            mx_pass(mb[:, 0, :], codes, scales, 0, 3, 4)
-            mx_pass(mb[:, 2, :], codes, scales, 1, 2, 3)
-            mx_pass(mb[:, 3, :], codes, scales, 2, 1, 2)
-            mx_pass(mb[:, 1, :], codes, scales, 3, 0, 1)
-            state[("mm", t)] = (ma, mb)
+            mm = mm_psum.tile([P, 4, Q], F32)
+            mx_pass(mm[:].rearrange("p n q -> p (n q)")[:, 0:2 * Q], codes, scales, 0, 1, 3)
+            mx_pass(mm[:, 2, :], codes, scales, 1, 0, 1)
+            mx_pass(mm[:, 3, :], codes, scales, 2, 0, 1)
+            state[("ma", t)] = mm
+            mm = mm_psum.tile([P, 4, Q], F32)
+            mx_pass(mm[:, 0, :], codes, scales, 0, 3, 4)
+            mx_pass(mm[:, 2, :], codes, scales, 1, 2, 3)
+            mx_pass(mm[:, 3, :], codes, scales, 2, 1, 2)
+            mx_pass(mm[:, 1, :], codes, scales, 3, 0, 1)
+            state[("mb", t)] = mm
 
         def exps(t):
-            ma, mb = state[("mm", t)]
+            ma, mb = state[("ma", t)], state[("mb", t)]
             sc = state[("s", t // OCT)]
             r = k = t % OCT
             if r == 0:
@@ -192,7 +215,7 @@ def tile_memorymoco_pa_t_kernel(tc, x0, x1, x2, x3, mem0, mem1, mem2, mem3, out)
                                  scale=sc[:, 3, k:k + 1])
 
         square_queue = [(t, v) for t in range(NT) for v in range(V)]
-        dot_queue = [(t, n) for t in range(NT) for n in range(len(PAIRS)) if n > 0 or t >= GRAM_STEPS]
+        dot_queue = [(t, n) for t in range(NT) for n in range(len(PAIRS)) if n == 3 or t >= GRAM_STEPS]
 
         def next_square():
             t, v = square_queue.pop(0)
@@ -200,9 +223,17 @@ def tile_memorymoco_pa_t_kernel(tc, x0, x1, x2, x3, mem0, mem1, mem2, mem3, out)
             if ("n2", b) not in state:
                 n2 = small.tile([P, V, OCT], F32)
                 state[("n2", b)] = n2
-            js = junk.tile([P, D], BF16)
-            nc.scalar.activation(out=js[:], in_=row_of(v, t), func=ACT.Square,
-                                 scale=sqrt_temp, accum_out=state[("n2", b)][:, v, k:k + 1])
+            if v >= (SHARED_AHEAD if t < LEAD else V - (t % SHARED_EVERY == 0)):
+                jv = junk.tile([P, D], BF16)
+                nc.vector.scalar_tensor_tensor(
+                    out=jv[:], in0=row_of(v, t), scalar=TEMP, in1=row_of(v, t),
+                    op0=ALU.mult, op1=ALU.mult, accum_out=state[("n2", b)][:, v, k:k + 1],
+                )
+                take_small()
+            else:
+                js = junk.tile([P, D], BF16)
+                nc.scalar.activation(out=js[:], in_=row_of(v, t), func=ACT.Square,
+                                     scale=sqrt_temp, accum_out=state[("n2", b)][:, v, k:k + 1])
 
         def dot_tile(t):
             b = t // OCT
@@ -299,21 +330,32 @@ def tile_memorymoco_pa_t_kernel(tc, x0, x1, x2, x3, mem0, mem1, mem2, mem3, out)
                 quantise("mem", mem_codes, mem_scales)
             if t == OCT:
                 scales_of(0)
+        transposes(0, [row_of(v, 0).bitcast(F32) for v in range(V)])
 
         cosine_step = {}
+        store_step = {}
         for c, (lo, hi) in enumerate(COLUMNS):
-            cosine_step[max(min(hi, GRAM_STEPS), DOTS_END - (NT - hi))] = c
+            step = max(min(hi, GRAM_STEPS) + 1, DOTS_END - (NT - hi))
+            cosine_step[step] = c
+            for piece in STORES:
+                if lo < piece[1] <= hi:
+                    store_step[piece] = max(piece[1], step) + 1
         batches_due = list(range(1, NT // OCT))
 
-        for i in range(-1, NT + 2):
+        for i in range(NT + 2):
+            if i < NT:
+                copy_out(i, (i in SCALAR_FIRST, i in SCALAR_SECOND))
+            if 0 <= i - 2 < GRAM_STEPS:
+                gram_dots(i - 2)
             if i + 1 < NT:
                 transposes(i + 1, [row_of(v, i + 1).bitcast(F32) for v in range(V)])
-            if 0 <= i < NT:
-                copy_out(i, (i in SCALAR_FIRST, i in SCALAR_SECOND))
-                if i < GRAM_STEPS:
-                    gram(i)
+            if i < GRAM_STEPS:
+                gram(i)
             if 0 <= i - 1 < NT:
                 quantise_step(i - 1)
+                if i - 1 < GRAM_STEPS:
+                    mask(i - 1)
+                    regroup(i - 1)
                 products(i - 1)
             if i in cosine_step:
                 cosines(cosine_step[i])
@@ -322,15 +364,12 @@ def tile_memorymoco_pa_t_kernel(tc, x0, x1, x2, x3, mem0, mem1, mem2, mem3, out)
             if i - 1 in cosine_step:
                 first_column(cosine_step[i - 1])
             for lo, hi in STORES:
-                if hi == i - 1:
+                if store_step[(lo, hi)] == i:
                     store(lo, hi)
-            if i >= 0:
-                squares_before = len(square_queue)
-                for n in range(share(len(square_queue), SQUARES_END - i)):
-                    next_square()
-                for n in range(share(len(dot_queue), DOTS_END - i)):
-                    next_dot()
-                if i < GRAM_STEPS:
-                    diagonal(i)
-                if batches_due and V * (NT - OCT * (batches_due[0] + 1)) >= squares_before:
-                    scales_of(batches_due.pop(0))
+            squares_before = len(square_queue)
+            for n in range(share(len(square_queue), SQUARES_END - i)):
+                next_square()
+            for n in range(share(len(dot_queue), DOTS_END - i)):
+                next_dot()
+            if batches_due and V * (NT - OCT * (batches_due[0] + 1)) >= squares_before:
+                scales_of(batches_due.pop(0))

@@ -27,17 +27,26 @@ NEWTON_STEPS = 3
 
 GROUPS = 4
 GROUP = P // GROUPS
-SHARED_AHEAD = 3
-SHARED_EVERY = 4
-LEAD = 9
+GRAM_STEPS = 24
+BATCHES = ((0, 8), (8, 16), (16, 20), (20, 24), (24, 32))
+WIDEST = max(hi - lo for lo, hi in BATCHES)
+BATCH_OF = [b for b, (lo, hi) in enumerate(BATCHES) for t in range(lo, hi)]
 COLUMNS = ((0, 8), (8, 16), (16, 20), (20, 24), (24, 28), (28, 32))
 STORES = ((0, 8), (8, 16), (16, 20), (20, 24), (24, 26), (26, 28), (28, 30), (30, 31), (31, 32))
-SQUARES_END = 22
-DOTS_AHEAD = 7
-SCALAR_FIRST = range(25, 29)
-SCALAR_SECOND = range(31, 31)
-DOTS_END = 28
-GRAM_STEPS = 25
+SQUARES_AHEAD = 9
+SQUARES_ALONE = 5
+SQUARES_BESIDE = 3
+DOTS_AHEAD = 1
+DOT_QUARTERS = 5
+DOTS_END = 32
+SCALAR_FIRST = range(28, 29)
+SCALAR_SECOND = range(28, 31)
+MEM_STEP = 0
+X_QUADS = 6
+HELD = 14
+EXPS_FROM = 13
+CATCH_UP = 23
+SMALL = 1
 
 FLOPS = 2 * NCOMBO * B * ROW * D
 
@@ -50,12 +59,13 @@ def tile_memorymoco_pa_t_kernel(tc, x0, x1, x2, x3, mem0, mem1, mem2, mem3, out)
     nc = tc.nc
     xs = (x0, x1, x2, x3)
     mems = (mem0, mem1, mem2, mem3)
-    sqrt_temp = TEMP ** 0.5
 
     with ExitStack() as ctx:
         keep = ctx.enter_context(tc.tile_pool(name="keep", bufs=1))
+        xpool = ctx.enter_context(tc.tile_pool(name="xpool", bufs=X_QUADS))
         opool = ctx.enter_context(tc.tile_pool(name="opool", bufs=2))
         work = ctx.enter_context(tc.tile_pool(name="work", bufs=3))
+        held = ctx.enter_context(tc.tile_pool(name="held", bufs=HELD))
         junk = ctx.enter_context(tc.tile_pool(name="junk", bufs=2))
         small = ctx.enter_context(tc.tile_pool(name="small", bufs=4))
         tp_psum = ctx.enter_context(tc.psum_pool(name="tp_psum", bufs=3))
@@ -65,17 +75,22 @@ def tile_memorymoco_pa_t_kernel(tc, x0, x1, x2, x3, mem0, mem1, mem2, mem3, out)
 
         mem_nat = keep.tile([P, V, D], BF16, name="mem_nat")
         xt = {}
-        for v in range(V):
-            for q in range(NT // QUAD):
-                xq = keep.tile([P, QUAD, D], BF16, name="x%d_%d" % (v, q))
-                xt[(v, q)] = xq
-        for lo, hi in ((0, 1), (1, 2), (2, 4)) + tuple((t, t + QUAD) for t in range(QUAD, NT, QUAD)):
+
+        def load(lo, hi):
             for v in range(V):
+                if lo % QUAD == 0:
+                    xq = xpool.tile([P, QUAD, D], BF16, name="x%d" % v)
+                    xt[(v, lo // QUAD)] = xq
                 src = xs[v].rearrange("(p t) d -> p t d", t=NT)
                 nc.sync.dma_start(out=xt[(v, lo // QUAD)][:, lo % QUAD:lo % QUAD + hi - lo, :], in_=src[:, lo:hi, :])
+
+        for lo, hi in ((0, 1), (1, 2), (2, 4)):
+            load(lo, hi)
             if lo == 1:
                 for j in range(V):
                     nc.sync.dma_start(out=mem_nat[:, j, :], in_=mems[j])
+        for q in range(1, X_QUADS):
+            load(QUAD * q, QUAD * q + QUAD)
 
         ident = keep.tile([P, P], F32, name="ident")
         make_identity(nc, ident[:])
@@ -102,8 +117,9 @@ def tile_memorymoco_pa_t_kernel(tc, x0, x1, x2, x3, mem0, mem1, mem2, mem3, out)
         pending = []
 
         def take_small():
-            if pending:
-                pending.pop(0)()
+            for n in range(SMALL):
+                if pending:
+                    pending.pop(0)()
 
         def row_of(v, t):
             return xt[(v, t // QUAD)][:, t % QUAD, :]
@@ -154,8 +170,10 @@ def tile_memorymoco_pa_t_kernel(tc, x0, x1, x2, x3, mem0, mem1, mem2, mem3, out)
             nc.tensor.matmul(state[("gm", t)][:, 1, 0:V], lhsT=state[("hd", t)][:], rhs=of_view[:],
                              start=True, stop=True)
 
-        def gram_dots(t):
-            nc.vector.tensor_copy(out=dot_tile(t)[:, 0:3, t % OCT], in_=state[("gm", t)][:, 1, 1:V])
+        def gram_stats(t):
+            nd, k = stats(t)
+            first = 0 if t < GRAM_STEPS else 1
+            nc.vector.tensor_copy(out=nd[:, V - 1 + first:V + 3, k], in_=state[("gm", t)][:, 1, first:V])
 
         def quantise(key, codes, scales):
             gt = state[("gt", key)]
@@ -167,8 +185,8 @@ def tile_memorymoco_pa_t_kernel(tc, x0, x1, x2, x3, mem0, mem1, mem2, mem3, out)
             take_small()
 
         def quantise_step(t):
-            codes = work.tile([P, V * P], U32, align_bytes=64)
-            scales = work.tile([P, V * P], U8, align_bytes=64)
+            codes = held.tile([P, V * P], U32, align_bytes=64)
+            scales = held.tile([P, V * P], U8, align_bytes=64)
             quantise(t, codes, scales)
             state[("cd", t)] = (codes, scales)
 
@@ -199,8 +217,10 @@ def tile_memorymoco_pa_t_kernel(tc, x0, x1, x2, x3, mem0, mem1, mem2, mem3, out)
 
         def exps(t):
             ma, mb = state[("ma", t)], state[("mb", t)]
-            sc = state[("s", t // OCT)]
-            r = k = t % OCT
+            b = BATCH_OF[t]
+            sc = state[("s", b)]
+            k = t - BATCHES[b][0]
+            r = t % OCT
             if r == 0:
                 ot = opool.tile([P, NCOMBO, OCT, ROW], F32)
                 state[("o", t // OCT)] = ot
@@ -214,74 +234,65 @@ def tile_memorymoco_pa_t_kernel(tc, x0, x1, x2, x3, mem0, mem1, mem2, mem3, out)
             nc.scalar.activation(out=ot[:, 4:7:2, r, 1:ROW], in_=mb[:, 2:4, :], func=ACT.Exp,
                                  scale=sc[:, 3, k:k + 1])
 
-        square_queue = [(t, v) for t in range(NT) for v in range(V)]
+        square_queue = [(t, v) for t in range(NT) for v in range(V) if v > 0 or t >= GRAM_STEPS]
         dot_queue = [(t, n) for t in range(NT) for n in range(len(PAIRS)) if n == 3 or t >= GRAM_STEPS]
+
+        def stats(t):
+            b = BATCH_OF[t]
+            if ("nd", b) not in state:
+                nd = small.tile([P, 2 * V, WIDEST], F32)
+                state[("nd", b)] = nd
+            return state[("nd", b)], t - BATCHES[b][0]
 
         def next_square():
             t, v = square_queue.pop(0)
-            b, k = t // OCT, t % OCT
-            if ("n2", b) not in state:
-                n2 = small.tile([P, V, OCT], F32)
-                state[("n2", b)] = n2
-            if v >= (SHARED_AHEAD if t < LEAD else V - (t % SHARED_EVERY == 0)):
-                jv = junk.tile([P, D], BF16)
-                nc.vector.scalar_tensor_tensor(
-                    out=jv[:], in0=row_of(v, t), scalar=TEMP, in1=row_of(v, t),
-                    op0=ALU.mult, op1=ALU.mult, accum_out=state[("n2", b)][:, v, k:k + 1],
-                )
-                take_small()
-            else:
-                js = junk.tile([P, D], BF16)
-                nc.scalar.activation(out=js[:], in_=row_of(v, t), func=ACT.Square,
-                                     scale=sqrt_temp, accum_out=state[("n2", b)][:, v, k:k + 1])
-
-        def dot_tile(t):
-            b = t // OCT
-            if ("dt", b) not in state:
-                dt = small.tile([P, len(PAIRS), OCT], F32)
-                state[("dt", b)] = dt
-            return state[("dt", b)]
+            nd, k = stats(t)
+            row = (v - 1) % V
+            js = junk.tile([P, D], BF16)
+            nc.scalar.activation(out=js[:], in_=row_of(v, t), func=ACT.Square, accum_out=nd[:, row, k:k + 1])
 
         def next_dot():
             t, n = dot_queue.pop(0)
-            dt = dot_tile(t)
-            k = t % OCT
+            nd, k = stats(t)
             i, j = PAIRS[n]
             jv = junk.tile([P, D], BF16)
             nc.vector.scalar_tensor_tensor(
                 out=jv[:], in0=row_of(i, t), scalar=1.0, in1=row_of(j, t),
-                op0=ALU.mult, op1=ALU.mult, accum_out=dt[:, n, k:k + 1],
+                op0=ALU.mult, op1=ALU.mult, accum_out=nd[:, V + n, k:k + 1],
             )
             take_small()
 
         def scales_of(b):
-            n2 = state[("n2", b)]
-            rn = small.tile([P, V, OCT], I32)
-            nw = small.tile([P, V, OCT], F32)
-            sc = small.tile([P, len(PAIRS), OCT], F32)
-            y = rn[:].bitcast(F32)
+            w = BATCHES[b][1] - BATCHES[b][0]
+            n2 = state[("nd", b)][:, 0:V, 0:w]
+            bits = state[("nd", b)][:].bitcast(I32)[:, 0:V, 0:w]
+            rn = small.tile([P, V, WIDEST], I32)
+            nw = small.tile([P, V, WIDEST], F32)
+            sc = small.tile([P, len(PAIRS), WIDEST], F32)
+            y = rn[:].bitcast(F32)[:, :, 0:w]
+            h = nw[:, :, 0:w]
 
             def guess():
-                nc.vector.tensor_scalar(out=rn[:], in0=n2[:].bitcast(I32), scalar1=-0.5, scalar2=RSQRT_BITS,
-                                        op0=ALU.mult, op1=ALU.add)
+                nc.vector.tensor_scalar(out=rn[:, :, 0:w], in0=bits, scalar1=-0.5,
+                                        scalar2=RSQRT_BITS, op0=ALU.mult, op1=ALU.add)
 
             def newton_a():
-                nc.vector.tensor_tensor(out=nw[:], in0=n2[:], in1=y, op=ALU.mult)
+                nc.vector.tensor_tensor(out=h, in0=n2, in1=y, op=ALU.mult)
 
             def newton_b():
-                nc.vector.scalar_tensor_tensor(out=nw[:], in0=nw[:], scalar=-0.5, in1=y,
-                                               op0=ALU.mult, op1=ALU.mult)
+                nc.vector.scalar_tensor_tensor(out=h, in0=h, scalar=-0.5, in1=y, op0=ALU.mult, op1=ALU.mult)
 
             def newton_c():
-                nc.vector.scalar_tensor_tensor(out=y, in0=nw[:], scalar=1.5, in1=y,
-                                               op0=ALU.add, op1=ALU.mult)
+                nc.vector.scalar_tensor_tensor(out=y, in0=h, scalar=1.5, in1=y, op0=ALU.add, op1=ALU.mult)
 
             def scale_a():
-                nc.vector.tensor_tensor(out=sc[:, 0:3, :], in0=y[:, 0:1, :].to_broadcast([P, 3, OCT]),
-                                        in1=y[:, 1:4, :], op=ALU.mult)
+                nc.vector.scalar_tensor_tensor(
+                    out=sc[:, 0:3, 0:w], in0=y[:, 0:3, :], scalar=1.0 / TEMP,
+                    in1=y[:, 3:4, :].to_broadcast([P, 3, w]), op0=ALU.mult, op1=ALU.mult)
 
             def scale_b():
-                nc.vector.tensor_tensor(out=sc[:, 3, :], in0=y[:, 1, :], in1=y[:, 2, :], op=ALU.mult)
+                nc.vector.scalar_tensor_tensor(out=sc[:, 3, 0:w], in0=y[:, 0, :], scalar=1.0 / TEMP,
+                                               in1=y[:, 1, :], op0=ALU.mult, op1=ALU.mult)
                 state[("s", b)] = sc
 
             pending.append(guess)
@@ -290,10 +301,11 @@ def tile_memorymoco_pa_t_kernel(tc, x0, x1, x2, x3, mem0, mem1, mem2, mem3, out)
 
         def cosines(c):
             lo, hi = COLUMNS[c]
-            b, r, w = lo // OCT, lo % OCT, hi - lo
+            b, w = BATCH_OF[lo], hi - lo
+            k = lo - BATCHES[b][0]
             zz = small.tile([P, len(PAIRS), OCT], F32)
-            nc.vector.tensor_tensor(out=zz[:, :, 0:w], in0=state[("dt", b)][:, :, r:r + w],
-                                    in1=state[("s", b)][:, :, r:r + w], op=ALU.mult)
+            nc.vector.tensor_tensor(out=zz[:, :, 0:w], in0=state[("nd", b)][:, V:2 * V, k:k + w],
+                                    in1=state[("s", b)][:, :, k:k + w], op=ALU.mult)
             state[("z", c)] = zz
 
         def first_column(c):
@@ -316,37 +328,28 @@ def tile_memorymoco_pa_t_kernel(tc, x0, x1, x2, x3, mem0, mem1, mem2, mem3, out)
                 in_=ot[:].rearrange("p c t q -> p c (t q)")[:, :, first:end],
             )
 
-        mem_words = mem_nat[:].bitcast(F32)
-        transposes("mem", [mem_words[:, j, :] for j in range(V)])
-        dots_left = len(dot_queue) - DOTS_AHEAD
-        for t in range(LEAD):
-            for v in range(V):
-                next_square()
-            for n in range(share(len(dot_queue) - dots_left, LEAD - t)):
-                next_dot()
-            if t == 1:
-                copy_out("mem", (False, False))
-            if t == 2:
-                quantise("mem", mem_codes, mem_scales)
-            if t == OCT:
-                scales_of(0)
         transposes(0, [row_of(v, 0).bitcast(F32) for v in range(V)])
+        batches_due = list(range(len(BATCHES)))
+        for n in range(max(SQUARES_AHEAD, DOTS_AHEAD)):
+            if n < SQUARES_AHEAD:
+                next_square()
+            if n < DOTS_AHEAD:
+                next_dot()
 
-        cosine_step = {}
-        store_step = {}
-        for c, (lo, hi) in enumerate(COLUMNS):
-            step = max(min(hi, GRAM_STEPS) + 1, DOTS_END - (NT - hi))
-            cosine_step[step] = c
-            for piece in STORES:
-                if lo < piece[1] <= hi:
-                    store_step[piece] = max(piece[1], step) + 1
-        batches_due = list(range(1, NT // OCT))
-
-        for i in range(NT + 2):
+        columns_due = list(range(len(COLUMNS)))
+        cosines_due = list(range(len(COLUMNS)))
+        stores_due = list(STORES)
+        columns_done = 0
+        scaled = 0
+        done = 0
+        i = 0
+        while stores_due:
+            if i % QUAD == 1 and X_QUADS + i // QUAD - 1 in range(X_QUADS, NT // QUAD):
+                load(QUAD * (X_QUADS + i // QUAD - 1), QUAD * (X_QUADS + i // QUAD))
             if i < NT:
                 copy_out(i, (i in SCALAR_FIRST, i in SCALAR_SECOND))
             if 0 <= i - 2 < GRAM_STEPS:
-                gram_dots(i - 2)
+                gram_stats(i - 2)
             if i + 1 < NT:
                 transposes(i + 1, [row_of(v, i + 1).bitcast(F32) for v in range(V)])
             if i < GRAM_STEPS:
@@ -356,20 +359,48 @@ def tile_memorymoco_pa_t_kernel(tc, x0, x1, x2, x3, mem0, mem1, mem2, mem3, out)
                 if i - 1 < GRAM_STEPS:
                     mask(i - 1)
                     regroup(i - 1)
-                products(i - 1)
-            if i in cosine_step:
-                cosines(cosine_step[i])
-            if 0 <= i - 2 < NT:
-                exps(i - 2)
-            if i - 1 in cosine_step:
-                first_column(cosine_step[i - 1])
-            for lo, hi in STORES:
-                if store_step[(lo, hi)] == i:
-                    store(lo, hi)
-            squares_before = len(square_queue)
-            for n in range(share(len(square_queue), SQUARES_END - i)):
-                next_square()
-            for n in range(share(len(dot_queue), DOTS_END - i)):
+            with_exps = False
+            for n in range(0 if i < EXPS_FROM else 1 if i < CATCH_UP else 2):
+                if done < min(i - 1, scaled):
+                    products(done)
+                    exps(done)
+                    done += 1
+                    with_exps = True
+            while columns_due and ("z", columns_due[0]) in state and COLUMNS[columns_due[0]][0] < done:
+                c = columns_due.pop(0)
+                first_column(c)
+                columns_done = COLUMNS[c][1]
+            while stores_due and stores_due[0][1] <= min(done, columns_done):
+                store(*stores_due.pop(0))
+            squared_before = square_queue[0][0] if square_queue else NT
+            for n in range(SQUARES_BESIDE if with_exps else SQUARES_ALONE):
+                if square_queue:
+                    next_square()
+            if i < GRAM_STEPS:
+                dots = (i + 1) * DOT_QUARTERS // 4 - i * DOT_QUARTERS // 4
+            else:
+                dots = share(len(dot_queue), DOTS_END - i)
+            for n in range(dots):
                 next_dot()
-            if batches_due and V * (NT - OCT * (batches_due[0] + 1)) >= squares_before:
-                scales_of(batches_due.pop(0))
+            if i == MEM_STEP:
+                mem_words = mem_nat[:].bitcast(F32)
+                transposes("mem", [mem_words[:, j, :] for j in range(V)])
+                copy_out("mem", (False, False))
+            if i == MEM_STEP + 1:
+                quantise("mem", mem_codes, mem_scales)
+            if i >= NT:
+                while pending:
+                    take_small()
+            for b, (lo, hi) in enumerate(BATCHES):
+                if ("s", b) in state and hi > scaled:
+                    scaled = hi
+            dotted = dot_queue[0][0] if dot_queue else NT
+            while cosines_due and COLUMNS[cosines_due[0]][1] <= min(scaled, dotted) and (
+                    i - 2 >= min(COLUMNS[cosines_due[0]][1], GRAM_STEPS) - 1):
+                cosines(cosines_due.pop(0))
+            if batches_due:
+                lo, hi = BATCHES[batches_due[0]]
+                last = min(hi, GRAM_STEPS) - 1
+                if squared_before >= hi and (lo >= GRAM_STEPS or i - 2 >= last):
+                    scales_of(batches_due.pop(0))
+            i += 1

@@ -22,31 +22,29 @@ ROW = Q + 1
 QUAD = 4
 OCT = 8
 PAIRS = ((0, 1), (0, 2), (0, 3), (1, 2))
-RSQRT_BITS = float(0x5F3759DF)
-NEWTON_STEPS = 3
-
 GROUPS = 4
 GROUP = P // GROUPS
-GRAM_STEPS = 24
-BATCHES = ((0, 8), (8, 16), (16, 20), (20, 24), (24, 32))
-WIDEST = max(hi - lo for lo, hi in BATCHES)
-BATCH_OF = [b for b, (lo, hi) in enumerate(BATCHES) for t in range(lo, hi)]
+GRAM_STEPS = 22
+BATCHES = ((0, 4), (4, 8), (8, 12), (12, 16), (16, 20), (20, 24), (24, 28), (28, 32))
 COLUMNS = ((0, 8), (8, 16), (16, 20), (20, 24), (24, 28), (28, 32))
 STORES = ((0, 8), (8, 16), (16, 20), (20, 24), (24, 26), (26, 28), (28, 30), (30, 31), (31, 32))
-SQUARES_AHEAD = 9
-SQUARES_ALONE = 5
-SQUARES_BESIDE = 3
-DOTS_AHEAD = 1
-DOT_QUARTERS = 5
-DOTS_END = 32
-SCALAR_FIRST = range(28, 29)
-SCALAR_SECOND = range(28, 31)
-MEM_STEP = 0
+SQUARES_AHEAD = 3
+SQUARES_ALONE = 24
+SQUARES_BESIDE = 14
+DOTS_AHEAD = 0
+DOT_QUARTERS = 9
+DOTS_END = 31
+SCALAR_FIRST = range(25, 25)
+SCALAR_SECOND = range(26, 28)
+MEM_STEP = 3
 X_QUADS = 6
-HELD = 14
-EXPS_FROM = 13
-CATCH_UP = 23
-SMALL = 1
+HELD = 11
+EXPS_FROM = 6
+CATCH_UP = 22
+TP_BANKS = 3
+SCALE_DELAY = 2
+SHARED = 1000
+PRE = True
 
 FLOPS = 2 * NCOMBO * B * ROW * D
 
@@ -68,9 +66,9 @@ def tile_memorymoco_pa_t_kernel(tc, x0, x1, x2, x3, mem0, mem1, mem2, mem3, out)
         held = ctx.enter_context(tc.tile_pool(name="held", bufs=HELD))
         junk = ctx.enter_context(tc.tile_pool(name="junk", bufs=2))
         small = ctx.enter_context(tc.tile_pool(name="small", bufs=4))
-        tp_psum = ctx.enter_context(tc.psum_pool(name="tp_psum", bufs=3))
+        tp_psum = ctx.enter_context(tc.psum_pool(name="tp_psum", bufs=TP_BANKS))
         gram_psum = ctx.enter_context(tc.psum_pool(name="gram_psum", bufs=2))
-        mm_psum = ctx.enter_context(tc.psum_pool(name="mm_psum", bufs=3))
+        mm_psum = ctx.enter_context(tc.psum_pool(name="mm_psum", bufs=6 - TP_BANKS))
         ctx.enter_context(tc.manual_schedule())
 
         mem_nat = keep.tile([P, V, D], BF16, name="mem_nat")
@@ -102,6 +100,8 @@ def tile_memorymoco_pa_t_kernel(tc, x0, x1, x2, x3, mem0, mem1, mem2, mem3, out)
                                 axis=mybir.AxisListType.X, op=ALU.add)
         on_diag = keep.tile([P, GROUP, GROUPS], F32, name="on_diag")
         nc.vector.tensor_copy(out=on_diag[:], in_=of_row[:].unsqueeze(2).to_broadcast([P, GROUP, GROUPS]))
+        neg_half = keep.tile([P, V, OCT], F32, name="neg_half")
+        nc.gpsimd.memset(neg_half[:], -0.5)
         warm_in = keep.tile([P, 1], F32, name="warm_in")
         warm_out = keep.tile([P, 1], F32, name="warm_out")
         nc.vector.memset(warm_in[:], 0.0)
@@ -113,13 +113,6 @@ def tile_memorymoco_pa_t_kernel(tc, x0, x1, x2, x3, mem0, mem1, mem2, mem3, out)
         out_view = out.rearrange("c (p t) q -> p c (t q)", t=NT)
 
         state = {}
-
-        pending = []
-
-        def take_small():
-            for n in range(SMALL):
-                if pending:
-                    pending.pop(0)()
 
         def row_of(v, t):
             return xt[(v, t // QUAD)][:, t % QUAD, :]
@@ -145,7 +138,6 @@ def tile_memorymoco_pa_t_kernel(tc, x0, x1, x2, x3, mem0, mem1, mem2, mem3, out)
                     nc.scalar.copy(out=dst, in_=src)
                 else:
                     nc.vector.tensor_copy(out=dst, in_=src)
-                    take_small()
             state[("gt", key)] = gt
 
         def gram(t):
@@ -163,7 +155,6 @@ def tile_memorymoco_pa_t_kernel(tc, x0, x1, x2, x3, mem0, mem1, mem2, mem3, out)
             nc.vector.tensor_tensor(
                 out=hd[:].rearrange("p (n g) -> p n g", g=GROUPS),
                 in0=gm[:, 0, :].rearrange("p (g n) -> p n g", g=GROUPS), in1=on_diag[:], op=ALU.mult)
-            take_small()
             state[("hd", t)] = hd
 
         def regroup(t):
@@ -182,7 +173,6 @@ def tile_memorymoco_pa_t_kernel(tc, x0, x1, x2, x3, mem0, mem1, mem2, mem3, out)
                 scales=scales[:],
                 in_=gt[:].rearrange("w n p j -> w (n p j)"),
             )
-            take_small()
 
         def quantise_step(t):
             codes = held.tile([P, V * P], U32, align_bytes=64)
@@ -217,10 +207,8 @@ def tile_memorymoco_pa_t_kernel(tc, x0, x1, x2, x3, mem0, mem1, mem2, mem3, out)
 
         def exps(t):
             ma, mb = state[("ma", t)], state[("mb", t)]
-            b = BATCH_OF[t]
-            sc = state[("s", b)]
-            k = t - BATCHES[b][0]
-            r = t % OCT
+            sc = state[("sc", t // OCT)]
+            r = k = t % OCT
             if r == 0:
                 ot = opool.tile([P, NCOMBO, OCT, ROW], F32)
                 state[("o", t // OCT)] = ot
@@ -238,18 +226,27 @@ def tile_memorymoco_pa_t_kernel(tc, x0, x1, x2, x3, mem0, mem1, mem2, mem3, out)
         dot_queue = [(t, n) for t in range(NT) for n in range(len(PAIRS)) if n == 3 or t >= GRAM_STEPS]
 
         def stats(t):
-            b = BATCH_OF[t]
-            if ("nd", b) not in state:
-                nd = small.tile([P, 2 * V, WIDEST], F32)
-                state[("nd", b)] = nd
-            return state[("nd", b)], t - BATCHES[b][0]
+            o = t // OCT
+            if ("nd", o) not in state:
+                nd = small.tile([P, 2 * V, OCT], F32)
+                rn = small.tile([P, V, OCT], F32)
+                sc = small.tile([P, len(PAIRS), OCT], F32)
+                state[("nd", o)], state[("rn", o)], state[("sc", o)] = nd, rn, sc
+            return state[("nd", o)], t % OCT
 
         def next_square():
             t, v = square_queue.pop(0)
             nd, k = stats(t)
             row = (v - 1) % V
-            js = junk.tile([P, D], BF16)
-            nc.scalar.activation(out=js[:], in_=row_of(v, t), func=ACT.Square, accum_out=nd[:, row, k:k + 1])
+            if len(square_queue) % SHARED == 1:
+                jv = junk.tile([P, D], BF16)
+                nc.vector.scalar_tensor_tensor(
+                    out=jv[:], in0=row_of(v, t), scalar=1.0, in1=row_of(v, t),
+                    op0=ALU.mult, op1=ALU.mult, accum_out=nd[:, row, k:k + 1],
+                )
+            else:
+                js = junk.tile([P, D], BF16)
+                nc.scalar.activation(out=js[:], in_=row_of(v, t), func=ACT.Square, accum_out=nd[:, row, k:k + 1])
 
         def next_dot():
             t, n = dot_queue.pop(0)
@@ -260,52 +257,32 @@ def tile_memorymoco_pa_t_kernel(tc, x0, x1, x2, x3, mem0, mem1, mem2, mem3, out)
                 out=jv[:], in0=row_of(i, t), scalar=1.0, in1=row_of(j, t),
                 op0=ALU.mult, op1=ALU.mult, accum_out=nd[:, V + n, k:k + 1],
             )
-            take_small()
+
+        def lengths_of(b):
+            lo, hi = BATCHES[b]
+            nd, k = stats(lo)
+            w = hi - lo
+            nc.gpsimd.tensor_tensor(out=state[("rn", lo // OCT)][:, :, k:k + w], in0=nd[:, 0:V, k:k + w],
+                                    in1=neg_half[:, :, 0:w], op=ALU.pow)
 
         def scales_of(b):
-            w = BATCHES[b][1] - BATCHES[b][0]
-            n2 = state[("nd", b)][:, 0:V, 0:w]
-            bits = state[("nd", b)][:].bitcast(I32)[:, 0:V, 0:w]
-            rn = small.tile([P, V, WIDEST], I32)
-            nw = small.tile([P, V, WIDEST], F32)
-            sc = small.tile([P, len(PAIRS), WIDEST], F32)
-            y = rn[:].bitcast(F32)[:, :, 0:w]
-            h = nw[:, :, 0:w]
+            lo, hi = BATCHES[b]
+            w, k, o = hi - lo, lo % OCT, lo // OCT
+            y = state[("rn", o)][:, :, k:k + w]
+            sc = state[("sc", o)]
 
-            def guess():
-                nc.vector.tensor_scalar(out=rn[:, :, 0:w], in0=bits, scalar1=-0.5,
-                                        scalar2=RSQRT_BITS, op0=ALU.mult, op1=ALU.add)
-
-            def newton_a():
-                nc.vector.tensor_tensor(out=h, in0=n2, in1=y, op=ALU.mult)
-
-            def newton_b():
-                nc.vector.scalar_tensor_tensor(out=h, in0=h, scalar=-0.5, in1=y, op0=ALU.mult, op1=ALU.mult)
-
-            def newton_c():
-                nc.vector.scalar_tensor_tensor(out=y, in0=h, scalar=1.5, in1=y, op0=ALU.add, op1=ALU.mult)
-
-            def scale_a():
-                nc.vector.scalar_tensor_tensor(
-                    out=sc[:, 0:3, 0:w], in0=y[:, 0:3, :], scalar=1.0 / TEMP,
-                    in1=y[:, 3:4, :].to_broadcast([P, 3, w]), op0=ALU.mult, op1=ALU.mult)
-
-            def scale_b():
-                nc.vector.scalar_tensor_tensor(out=sc[:, 3, 0:w], in0=y[:, 0, :], scalar=1.0 / TEMP,
-                                               in1=y[:, 1, :], op0=ALU.mult, op1=ALU.mult)
-                state[("s", b)] = sc
-
-            pending.append(guess)
-            pending.extend([newton_a, newton_b, newton_c] * NEWTON_STEPS)
-            pending.extend([scale_a, scale_b])
+            nc.vector.scalar_tensor_tensor(
+                out=sc[:, 0:3, k:k + w], in0=y[:, 0:3, :], scalar=1.0 / TEMP,
+                in1=y[:, 3:4, :].to_broadcast([P, 3, w]), op0=ALU.mult, op1=ALU.mult)
+            nc.vector.scalar_tensor_tensor(out=sc[:, 3, k:k + w], in0=y[:, 0, :], scalar=1.0 / TEMP,
+                                           in1=y[:, 1, :], op0=ALU.mult, op1=ALU.mult)
 
         def cosines(c):
             lo, hi = COLUMNS[c]
-            b, w = BATCH_OF[lo], hi - lo
-            k = lo - BATCHES[b][0]
+            o, k, w = lo // OCT, lo % OCT, hi - lo
             zz = small.tile([P, len(PAIRS), OCT], F32)
-            nc.vector.tensor_tensor(out=zz[:, :, 0:w], in0=state[("nd", b)][:, V:2 * V, k:k + w],
-                                    in1=state[("s", b)][:, :, k:k + w], op=ALU.mult)
+            nc.vector.tensor_tensor(out=zz[:, :, 0:w], in0=state[("nd", o)][:, V:2 * V, k:k + w],
+                                    in1=state[("sc", o)][:, :, k:k + w], op=ALU.mult)
             state[("z", c)] = zz
 
         def first_column(c):
@@ -341,8 +318,10 @@ def tile_memorymoco_pa_t_kernel(tc, x0, x1, x2, x3, mem0, mem1, mem2, mem3, out)
         stores_due = list(STORES)
         columns_done = 0
         scaled = 0
+        multiplied = 0
         done = 0
         i = 0
+        scales_due = []
         while stores_due:
             if i % QUAD == 1 and X_QUADS + i // QUAD - 1 in range(X_QUADS, NT // QUAD):
                 load(QUAD * (X_QUADS + i // QUAD - 1), QUAD * (X_QUADS + i // QUAD))
@@ -359,9 +338,21 @@ def tile_memorymoco_pa_t_kernel(tc, x0, x1, x2, x3, mem0, mem1, mem2, mem3, out)
                 if i - 1 < GRAM_STEPS:
                     mask(i - 1)
                     regroup(i - 1)
+            while scales_due and scales_due[0][0] == i:
+                b = scales_due.pop(0)[1]
+                scales_of(b)
+                scaled = BATCHES[b][1]
             with_exps = False
             for n in range(0 if i < EXPS_FROM else 1 if i < CATCH_UP else 2):
-                if done < min(i - 1, scaled):
+                if PRE:
+                    if done < multiplied:
+                        exps(done)
+                        done += 1
+                        with_exps = True
+                    if multiplied < min(i - 1, scaled) and multiplied < done + 1:
+                        products(multiplied)
+                        multiplied += 1
+                elif done < min(i - 1, scaled):
                     products(done)
                     exps(done)
                     done += 1
@@ -373,7 +364,8 @@ def tile_memorymoco_pa_t_kernel(tc, x0, x1, x2, x3, mem0, mem1, mem2, mem3, out)
             while stores_due and stores_due[0][1] <= min(done, columns_done):
                 store(*stores_due.pop(0))
             squared_before = square_queue[0][0] if square_queue else NT
-            for n in range(SQUARES_BESIDE if with_exps else SQUARES_ALONE):
+            quarters = SQUARES_BESIDE if with_exps else SQUARES_ALONE
+            for n in range((i + 1) * quarters // 4 - i * quarters // 4):
                 if square_queue:
                     next_square()
             if i < GRAM_STEPS:
@@ -388,12 +380,6 @@ def tile_memorymoco_pa_t_kernel(tc, x0, x1, x2, x3, mem0, mem1, mem2, mem3, out)
                 copy_out("mem", (False, False))
             if i == MEM_STEP + 1:
                 quantise("mem", mem_codes, mem_scales)
-            if i >= NT:
-                while pending:
-                    take_small()
-            for b, (lo, hi) in enumerate(BATCHES):
-                if ("s", b) in state and hi > scaled:
-                    scaled = hi
             dotted = dot_queue[0][0] if dot_queue else NT
             while cosines_due and COLUMNS[cosines_due[0]][1] <= min(scaled, dotted) and (
                     i - 2 >= min(COLUMNS[cosines_due[0]][1], GRAM_STEPS) - 1):
@@ -402,5 +388,7 @@ def tile_memorymoco_pa_t_kernel(tc, x0, x1, x2, x3, mem0, mem1, mem2, mem3, out)
                 lo, hi = BATCHES[batches_due[0]]
                 last = min(hi, GRAM_STEPS) - 1
                 if squared_before >= hi and (lo >= GRAM_STEPS or i - 2 >= last):
-                    scales_of(batches_due.pop(0))
+                    b = batches_due.pop(0)
+                    lengths_of(b)
+                    scales_due.append((i + SCALE_DELAY, b))
             i += 1

@@ -24,26 +24,29 @@ OCT = 8
 PAIRS = ((0, 1), (0, 2), (0, 3), (1, 2))
 GROUPS = 4
 GROUP = P // GROUPS
-GRAM_STEPS = 22
+GRAM_STEPS = 25
+GRAM_LENGTHS = 21
 BATCHES = ((0, 4), (4, 8), (8, 12), (12, 16), (16, 20), (20, 24), (24, 28), (28, 32))
-COLUMNS = ((0, 8), (8, 16), (16, 20), (20, 24), (24, 28), (28, 32))
-STORES = ((0, 8), (8, 16), (16, 20), (20, 24), (24, 26), (26, 28), (28, 30), (30, 31), (31, 32))
+COLUMNS = ((0, 8), (8, 12), (12, 16), (16, 20), (20, 24), (24, 28), (28, 32))
+STORES = ((0, 8), (8, 12), (12, 16), (16, 20), (20, 24), (24, 26), (26, 28), (28, 30), (30, 31))
 SQUARES_AHEAD = 3
-SQUARES_ALONE = 24
-SQUARES_BESIDE = 14
-DOTS_AHEAD = 0
-DOT_QUARTERS = 9
+SQUARES_ALONE = 25
+SQUARES_BESIDE = 13
+DOTS_AHEAD = 1
+DOT_QUARTERS = 5
 DOTS_END = 31
-SCALAR_FIRST = range(25, 25)
-SCALAR_SECOND = range(26, 28)
+SCALAR_FIRST = range(29, 30)
+SCALAR_SECOND = range(26, 31)
 MEM_STEP = 3
+LOAD_ORDER = (1, 0, 2, 3)
+FIRST_LOADS = ((0, 1), (1, 2), (2, 4), (4, 8))
 X_QUADS = 6
 HELD = 11
-EXPS_FROM = 6
-CATCH_UP = 22
+EXPS_FROM = 7
+CATCH_UP = 24
 TP_BANKS = 3
 SCALE_DELAY = 2
-SHARED = 1000
+SHARED = 12
 PRE = True
 
 FLOPS = 2 * NCOMBO * B * ROW * D
@@ -75,19 +78,18 @@ def tile_memorymoco_pa_t_kernel(tc, x0, x1, x2, x3, mem0, mem1, mem2, mem3, out)
         xt = {}
 
         def load(lo, hi):
-            for v in range(V):
+            for v in LOAD_ORDER:
                 if lo % QUAD == 0:
                     xq = xpool.tile([P, QUAD, D], BF16, name="x%d" % v)
                     xt[(v, lo // QUAD)] = xq
                 src = xs[v].rearrange("(p t) d -> p t d", t=NT)
                 nc.sync.dma_start(out=xt[(v, lo // QUAD)][:, lo % QUAD:lo % QUAD + hi - lo, :], in_=src[:, lo:hi, :])
 
-        for lo, hi in ((0, 1), (1, 2), (2, 4)):
+        for lo, hi in FIRST_LOADS:
             load(lo, hi)
-            if lo == 1:
-                for j in range(V):
-                    nc.sync.dma_start(out=mem_nat[:, j, :], in_=mems[j])
-        for q in range(1, X_QUADS):
+        for j in range(V):
+            nc.sync.dma_start(out=mem_nat[:, j, :], in_=mems[j])
+        for q in range(FIRST_LOADS[-1][1] // QUAD, X_QUADS):
             load(QUAD * q, QUAD * q + QUAD)
 
         ident = keep.tile([P, P], F32, name="ident")
@@ -163,8 +165,8 @@ def tile_memorymoco_pa_t_kernel(tc, x0, x1, x2, x3, mem0, mem1, mem2, mem3, out)
 
         def gram_stats(t):
             nd, k = stats(t)
-            first = 0 if t < GRAM_STEPS else 1
-            nc.vector.tensor_copy(out=nd[:, V - 1 + first:V + 3, k], in_=state[("gm", t)][:, 1, first:V])
+            first = 0 if t < GRAM_LENGTHS else 1
+            nc.vector.tensor_copy(out=nd[:, V - 1 + first:2 * V - 1, k], in_=state[("gm", t)][:, 1, first:V])
 
         def quantise(key, codes, scales):
             gt = state[("gt", key)]
@@ -213,16 +215,18 @@ def tile_memorymoco_pa_t_kernel(tc, x0, x1, x2, x3, mem0, mem1, mem2, mem3, out)
                 ot = opool.tile([P, NCOMBO, OCT, ROW], F32)
                 state[("o", t // OCT)] = ot
             ot = state[("o", t // OCT)]
-            nc.scalar.activation(out=ot[:, 1:6:4, r, 1:ROW], in_=ma[:, 1:4:2, :], func=ACT.Exp,
-                                 scale=sc[:, 1, k:k + 1])
-            nc.scalar.activation(out=ot[:, 0:4:3, r, 1:ROW], in_=ma[:, 0:3:2, :], func=ACT.Exp,
-                                 scale=sc[:, 0, k:k + 1])
-            nc.scalar.activation(out=ot[:, 2:8:5, r, 1:ROW], in_=mb[:, 0:2, :], func=ACT.Exp,
-                                 scale=sc[:, 2, k:k + 1])
-            nc.scalar.activation(out=ot[:, 4:7:2, r, 1:ROW], in_=mb[:, 2:4, :], func=ACT.Exp,
-                                 scale=sc[:, 3, k:k + 1])
+            for combos, bank, columns, pair in (
+                (slice(1, 6, 4), ma, slice(1, 4, 2), 1), (slice(0, 4, 3), ma, slice(0, 3, 2), 0),
+                (slice(2, 8, 5), mb, slice(0, 2), 2), (slice(4, 7, 2), mb, slice(2, 4), 3),
+            ):
+                nc.scalar.activation(out=ot[:, combos, r, 1:ROW], in_=bank[:, columns, :], func=ACT.Exp,
+                                     scale=sc[:, pair, k:k + 1])
+                if t == NT - 1:
+                    store(NT - 1, NT, combos)
 
-        square_queue = [(t, v) for t in range(NT) for v in range(V) if v > 0 or t >= GRAM_STEPS]
+        arrivals = FIRST_LOADS + tuple((t, t + QUAD) for t in range(FIRST_LOADS[-1][1], NT, QUAD))
+        square_queue = [(t, v) for lo, hi in arrivals for v in LOAD_ORDER for t in range(lo, hi)
+                        if v > 0 or t >= GRAM_LENGTHS]
         dot_queue = [(t, n) for t in range(NT) for n in range(len(PAIRS)) if n == 3 or t >= GRAM_STEPS]
 
         def stats(t):
@@ -295,14 +299,14 @@ def tile_memorymoco_pa_t_kernel(tc, x0, x1, x2, x3, mem0, mem1, mem2, mem3, out)
             nc.scalar.activation(out=ot[:, 4:7:2, r:r + w, 0],
                                  in_=zz[:, 3:4, 0:w].to_broadcast([P, 2, w]), func=ACT.Exp)
 
-        def store(lo, hi):
+        def store(lo, hi, combos=slice(0, NCOMBO)):
             o = lo // OCT
             ot = state[("o", o)]
             first = Q * (lo - o * OCT)
             end = OCT * ROW if hi == (o + 1) * OCT else Q * (hi - o * OCT)
             nc.sync.dma_start(
-                out=out_view[:, :, o * OCT * ROW + first:o * OCT * ROW + end],
-                in_=ot[:].rearrange("p c t q -> p c (t q)")[:, :, first:end],
+                out=out_view[:, combos, o * OCT * ROW + first:o * OCT * ROW + end],
+                in_=ot[:].rearrange("p c t q -> p c (t q)")[:, combos, first:end],
             )
 
         transposes(0, [row_of(v, 0).bitcast(F32) for v in range(V)])
@@ -322,7 +326,7 @@ def tile_memorymoco_pa_t_kernel(tc, x0, x1, x2, x3, mem0, mem1, mem2, mem3, out)
         done = 0
         i = 0
         scales_due = []
-        while stores_due:
+        while done < NT:
             if i % QUAD == 1 and X_QUADS + i // QUAD - 1 in range(X_QUADS, NT // QUAD):
                 load(QUAD * (X_QUADS + i // QUAD - 1), QUAD * (X_QUADS + i // QUAD))
             if i < NT:
@@ -363,7 +367,7 @@ def tile_memorymoco_pa_t_kernel(tc, x0, x1, x2, x3, mem0, mem1, mem2, mem3, out)
                 columns_done = COLUMNS[c][1]
             while stores_due and stores_due[0][1] <= min(done, columns_done):
                 store(*stores_due.pop(0))
-            squared_before = square_queue[0][0] if square_queue else NT
+            squared_before = min([t for t, v in square_queue] + [NT])
             quarters = SQUARES_BESIDE if with_exps else SQUARES_ALONE
             for n in range((i + 1) * quarters // 4 - i * quarters // 4):
                 if square_queue:
@@ -372,7 +376,7 @@ def tile_memorymoco_pa_t_kernel(tc, x0, x1, x2, x3, mem0, mem1, mem2, mem3, out)
                 dots = (i + 1) * DOT_QUARTERS // 4 - i * DOT_QUARTERS // 4
             else:
                 dots = share(len(dot_queue), DOTS_END - i)
-            for n in range(dots):
+            for n in range(min(dots, len(dot_queue))):
                 next_dot()
             if i == MEM_STEP:
                 mem_words = mem_nat[:].bitcast(F32)
@@ -386,8 +390,8 @@ def tile_memorymoco_pa_t_kernel(tc, x0, x1, x2, x3, mem0, mem1, mem2, mem3, out)
                 cosines(cosines_due.pop(0))
             if batches_due:
                 lo, hi = BATCHES[batches_due[0]]
-                last = min(hi, GRAM_STEPS) - 1
-                if squared_before >= hi and (lo >= GRAM_STEPS or i - 2 >= last):
+                last = min(hi, GRAM_LENGTHS) - 1
+                if squared_before >= hi and (lo >= GRAM_LENGTHS or i - 2 >= last):
                     b = batches_due.pop(0)
                     lengths_of(b)
                     scales_due.append((i + SCALE_DELAY, b))

@@ -27,16 +27,16 @@ GROUP = P // GROUPS
 GRAM_STEPS = 25
 GRAM_LENGTHS = 21
 BATCHES = ((0, 4), (4, 8), (8, 12), (12, 16), (16, 20), (20, 24), (24, 28), (28, 32))
-COLUMNS = ((0, 8), (8, 12), (12, 16), (16, 20), (20, 24), (24, 28), (28, 32))
+COLUMNS = ((0, 8), (8, 16), (16, 20), (20, 24), (24, 28), (28, 32))
 STORES = ((0, 8), (8, 12), (12, 16), (16, 20), (20, 24), (24, 26), (26, 28), (28, 30), (30, 31))
-SQUARES_AHEAD = 3
-SQUARES_ALONE = 25
-SQUARES_BESIDE = 13
-DOTS_AHEAD = 1
-DOT_QUARTERS = 5
+SQUARES_AHEAD = 9
+SQUARES_ALONE = 24
+SQUARES_BESIDE = 12
+DOTS_AHEAD = 0
+DOT_QUARTERS = 6
 DOTS_END = 31
-SCALAR_FIRST = range(29, 30)
-SCALAR_SECOND = range(26, 31)
+SCALAR_FIRST = range(29, 29)
+SCALAR_SECOND = range(26, 29)
 MEM_STEP = 3
 LOAD_ORDER = (1, 0, 2, 3)
 FIRST_LOADS = ((0, 1), (1, 2), (2, 4), (4, 8))
@@ -46,7 +46,7 @@ EXPS_FROM = 7
 CATCH_UP = 24
 TP_BANKS = 3
 SCALE_DELAY = 2
-SHARED = 12
+SHARED = 30
 PRE = True
 
 FLOPS = 2 * NCOMBO * B * ROW * D
@@ -122,7 +122,10 @@ def tile_memorymoco_pa_t_kernel(tc, x0, x1, x2, x3, mem0, mem1, mem2, mem3, out)
         def transposes(key, sources):
             banks = []
             for h in range(2):
-                tp = tp_psum.tile([P, 2, 2, P], F32)
+                if key == "mem":
+                    tp = mm_psum.tile([P, 2, 2, P], F32, name="mm")
+                else:
+                    tp = tp_psum.tile([P, 2, 2, P], F32)
                 for v in (2 * h, 2 * h + 1):
                     for u in range(2):
                         nc.tensor.transpose(tp[:, v % 2, u, :], sources[v][:, u:2 * P:2], ident[:])
@@ -131,7 +134,10 @@ def tile_memorymoco_pa_t_kernel(tc, x0, x1, x2, x3, mem0, mem1, mem2, mem3, out)
 
         def copy_out(key, on_scalar):
             banks = state[("tp", key)]
-            gt = work.tile([P, V, P, 4], BF16, align_bytes=64)
+            if key == "mem":
+                gt = keep.tile([P, V, P, 4], BF16, name="gtm", align_bytes=64)
+            else:
+                gt = work.tile([P, V, P, 4], BF16, align_bytes=64)
             gtw = gt[:].bitcast(F32)
             for h in range(2):
                 dst = gtw[:, 2 * h:2 * h + 2, :, :]
@@ -381,8 +387,9 @@ def tile_memorymoco_pa_t_kernel(tc, x0, x1, x2, x3, mem0, mem1, mem2, mem3, out)
             if i == MEM_STEP:
                 mem_words = mem_nat[:].bitcast(F32)
                 transposes("mem", [mem_words[:, j, :] for j in range(V)])
-                copy_out("mem", (False, False))
             if i == MEM_STEP + 1:
+                copy_out("mem", (False, False))
+            if i == MEM_STEP + 2:
                 quantise("mem", mem_codes, mem_scales)
             dotted = dot_queue[0][0] if dot_queue else NT
             while cosines_due and COLUMNS[cosines_due[0]][1] <= min(scaled, dotted) and (

@@ -7,7 +7,6 @@ BF16 = mybir.dt.bfloat16
 F32 = mybir.dt.float32
 U32 = mybir.dt.uint32
 U8 = mybir.dt.uint8
-I32 = mybir.dt.int32
 FP8X4 = mybir.dt.float8_e4m3fn_x4
 ACT = mybir.ActivationFunctionType
 ALU = mybir.AluOpType
@@ -15,41 +14,43 @@ ALU = mybir.AluOpType
 P = 128
 B, Q, D = 4096, 128, 512
 V = 4
-NT = B // P
+STEPS = B // P
 TEMP = 0.07
-NCOMBO = 8
+COMBOS = 8
 ROW = Q + 1
+PACK = 4
 QUAD = 4
 OCT = 8
 PAIRS = ((0, 1), (0, 2), (0, 3), (1, 2))
+
 GROUPS = 4
 GROUP = P // GROUPS
 GRAM_STEPS = 25
 GRAM_LENGTHS = 21
-BATCHES = ((0, 4), (4, 8), (8, 12), (12, 16), (16, 20), (20, 24), (24, 28), (28, 32))
-COLUMNS = ((0, 8), (8, 16), (16, 20), (20, 24), (24, 28), (28, 32))
-STORES = ((0, 8), (8, 12), (12, 16), (16, 20), (20, 24), (24, 26), (26, 28), (28, 30), (30, 31))
-SQUARES_AHEAD = 9
-SQUARES_ALONE = 24
-SQUARES_BESIDE = 12
-DOTS_AHEAD = 0
-DOT_QUARTERS = 6
-DOTS_END = 31
-SCALAR_FIRST = range(29, 29)
-SCALAR_SECOND = range(26, 29)
-MEM_STEP = 3
-LOAD_ORDER = (1, 0, 2, 3)
+
 FIRST_LOADS = ((0, 1), (1, 2), (2, 4), (4, 8))
+LATER_LOADS = tuple((t, t + QUAD) for t in range(FIRST_LOADS[-1][1], STEPS, QUAD))
+LOAD_ORDER = (1, 0, 2, 3)
 X_QUADS = 6
 HELD = 11
-EXPS_FROM = 7
-CATCH_UP = 24
-TP_BANKS = 3
-SCALE_DELAY = 2
-SHARED = 30
-PRE = True
 
-FLOPS = 2 * NCOMBO * B * ROW * D
+SQUARES_AHEAD = 12
+SQUARES_ALONE = 9
+SQUARES_BESIDE = 7
+VECTOR_SQUARE = 4
+DOTS_AHEAD = 1
+DOTS_IN_TWO = 3
+DOTS_END = 31
+EXPS_FROM = 7
+TWO_EXPS_FROM = 24
+MEMORY_STEP = 2
+SCALAR_COPIES = range(28, 31)
+SCALES_AFTER = 2
+
+COLUMNS = ((0, 8), (8, 16), (16, 20), (20, 24), (24, 28), (28, 30), (30, 32))
+STORES = ((0, 8), (8, 12), (12, 16), (16, 20), (20, 22), (22, 24), (24, 26), (26, 28), (28, 29), (29, 30), (30, 31))
+
+FLOPS = 2 * COMBOS * B * ROW * D
 
 
 def share(left, steps):
@@ -58,39 +59,44 @@ def share(left, steps):
 
 def tile_memorymoco_pa_t_kernel(tc, x0, x1, x2, x3, mem0, mem1, mem2, mem3, out):
     nc = tc.nc
-    xs = (x0, x1, x2, x3)
-    mems = (mem0, mem1, mem2, mem3)
+    views = [x.rearrange("(p t) d -> p t d", t=STEPS) for x in (x0, x1, x2, x3)]
+    memories = (mem0, mem1, mem2, mem3)
+    out_view = out.rearrange("c (p t) q -> p c (t q)", t=STEPS)
 
     with ExitStack() as ctx:
         keep = ctx.enter_context(tc.tile_pool(name="keep", bufs=1))
-        xpool = ctx.enter_context(tc.tile_pool(name="xpool", bufs=X_QUADS))
-        opool = ctx.enter_context(tc.tile_pool(name="opool", bufs=2))
+        row_pool = ctx.enter_context(tc.tile_pool(name="row_pool", bufs=X_QUADS))
+        out_pool = ctx.enter_context(tc.tile_pool(name="out_pool", bufs=2))
         work = ctx.enter_context(tc.tile_pool(name="work", bufs=3))
         held = ctx.enter_context(tc.tile_pool(name="held", bufs=HELD))
-        junk = ctx.enter_context(tc.tile_pool(name="junk", bufs=2))
+        unread = ctx.enter_context(tc.tile_pool(name="unread", bufs=2))
         small = ctx.enter_context(tc.tile_pool(name="small", bufs=4))
-        tp_psum = ctx.enter_context(tc.psum_pool(name="tp_psum", bufs=TP_BANKS))
+        transpose_psum = ctx.enter_context(tc.psum_pool(name="transpose_psum", bufs=3))
         gram_psum = ctx.enter_context(tc.psum_pool(name="gram_psum", bufs=2))
-        mm_psum = ctx.enter_context(tc.psum_pool(name="mm_psum", bufs=6 - TP_BANKS))
+        product_psum = ctx.enter_context(tc.psum_pool(name="product_psum", bufs=3))
         ctx.enter_context(tc.manual_schedule())
 
-        mem_nat = keep.tile([P, V, D], BF16, name="mem_nat")
-        xt = {}
+        memory_rows = keep.tile([P, V, D], BF16, name="memory_rows")
+        quads = {}
 
-        def load(lo, hi):
+        def load(first, end):
             for v in LOAD_ORDER:
-                if lo % QUAD == 0:
-                    xq = xpool.tile([P, QUAD, D], BF16, name="x%d" % v)
-                    xt[(v, lo // QUAD)] = xq
-                src = xs[v].rearrange("(p t) d -> p t d", t=NT)
-                nc.sync.dma_start(out=xt[(v, lo // QUAD)][:, lo % QUAD:lo % QUAD + hi - lo, :], in_=src[:, lo:hi, :])
+                q = first // QUAD
+                if first % QUAD == 0:
+                    rows = row_pool.tile([P, QUAD, D], BF16, name="rows%d" % v)
+                    quads[(v, q)] = rows
+                nc.sync.dma_start(out=quads[(v, q)][:, first - QUAD * q:end - QUAD * q, :],
+                                  in_=views[v][:, first:end, :])
 
-        for lo, hi in FIRST_LOADS:
-            load(lo, hi)
+        def row_of(v, t):
+            return quads[(v, t // QUAD)][:, t % QUAD, :]
+
+        for first, end in FIRST_LOADS:
+            load(first, end)
         for j in range(V):
-            nc.sync.dma_start(out=mem_nat[:, j, :], in_=mems[j])
-        for q in range(FIRST_LOADS[-1][1] // QUAD, X_QUADS):
-            load(QUAD * q, QUAD * q + QUAD)
+            nc.sync.dma_start(out=memory_rows[:, j, :], in_=memories[j])
+        for first, end in LATER_LOADS[:X_QUADS - FIRST_LOADS[-1][1] // QUAD]:
+            load(first, end)
 
         ident = keep.tile([P, P], F32, name="ident")
         make_identity(nc, ident[:])
@@ -100,8 +106,8 @@ def tile_memorymoco_pa_t_kernel(tc, x0, x1, x2, x3, mem0, mem1, mem2, mem3, out)
         of_row = keep.tile([P, GROUP], F32, name="of_row")
         nc.vector.tensor_reduce(out=of_row[:], in_=ident[:].rearrange("p (v r) -> p r v", v=V),
                                 axis=mybir.AxisListType.X, op=ALU.add)
-        on_diag = keep.tile([P, GROUP, GROUPS], F32, name="on_diag")
-        nc.vector.tensor_copy(out=on_diag[:], in_=of_row[:].unsqueeze(2).to_broadcast([P, GROUP, GROUPS]))
+        on_diagonal = keep.tile([P, GROUP, GROUPS], F32, name="on_diagonal")
+        nc.vector.tensor_copy(out=on_diagonal[:], in_=of_row[:].unsqueeze(2).to_broadcast([P, GROUP, GROUPS]))
         neg_half = keep.tile([P, V, OCT], F32, name="neg_half")
         nc.gpsimd.memset(neg_half[:], -0.5)
         warm_in = keep.tile([P, 1], F32, name="warm_in")
@@ -109,297 +115,272 @@ def tile_memorymoco_pa_t_kernel(tc, x0, x1, x2, x3, mem0, mem1, mem2, mem3, out)
         nc.vector.memset(warm_in[:], 0.0)
         nc.scalar.activation(out=warm_out[:], in_=warm_in[:], func=ACT.Exp)
 
-        mem_codes = keep.tile([P, V * Q], U32, name="mem_codes", align_bytes=64)
-        mem_scales = keep.tile([P, V * Q], U8, name="mem_scales", align_bytes=64)
+        memory_codes = keep.tile([P, V * Q], U32, name="memory_codes", align_bytes=64)
+        memory_scales = keep.tile([P, V * Q], U8, name="memory_scales", align_bytes=64)
 
-        out_view = out.rearrange("c (p t) q -> p c (t q)", t=NT)
-
-        state = {}
-
-        def row_of(v, t):
-            return xt[(v, t // QUAD)][:, t % QUAD, :]
-
-        def transposes(key, sources):
+        def transposes(pool, name, sources):
             banks = []
             for h in range(2):
-                if key == "mem":
-                    tp = mm_psum.tile([P, 2, 2, P], F32, name="mm")
-                else:
-                    tp = tp_psum.tile([P, 2, 2, P], F32)
+                bank = pool.tile([P, 2, 2, P], F32, name=name)
                 for v in (2 * h, 2 * h + 1):
                     for u in range(2):
-                        nc.tensor.transpose(tp[:, v % 2, u, :], sources[v][:, u:2 * P:2], ident[:])
-                banks.append(tp)
-            state[("tp", key)] = banks
+                        nc.tensor.transpose(bank[:, v % 2, u, :], sources[v].bitcast(F32)[:, u:2 * P:2], ident[:])
+                banks.append(bank)
+            return banks
 
-        def copy_out(key, on_scalar):
-            banks = state[("tp", key)]
-            if key == "mem":
-                gt = keep.tile([P, V, P, 4], BF16, name="gtm", align_bytes=64)
-            else:
-                gt = work.tile([P, V, P, 4], BF16, align_bytes=64)
-            gtw = gt[:].bitcast(F32)
+        def copy_out(banks, grouped, engines):
+            words = grouped[:].bitcast(F32)
             for h in range(2):
-                dst = gtw[:, 2 * h:2 * h + 2, :, :]
-                src = banks[h][:].rearrange("w n u p -> w n p u")
-                if on_scalar[h]:
-                    nc.scalar.copy(out=dst, in_=src)
-                else:
-                    nc.vector.tensor_copy(out=dst, in_=src)
-            state[("gt", key)] = gt
+                engines[h](out=words[:, 2 * h:2 * h + 2, :, :], in_=banks[h][:].rearrange("w n u p -> w n p u"))
 
-        def gram(t):
-            columns = state[("gt", t)][:].rearrange("w v p j -> w (v p) j")
-            gm = gram_psum.tile([P, GROUPS, P], F32)
-            for g in range(GROUPS):
-                for j in range(4):
-                    nc.tensor.matmul(gm[:, 0, GROUP * g:GROUP * g + GROUP], lhsT=columns[:, g:V * P:GROUPS, j],
-                                     rhs=columns[:, g:P:GROUPS, j], start=(j == 0), stop=(j == 3))
-            state[("gm", t)] = gm
+        def quantise(grouped, codes, scales):
+            nc.vector.quantize_mx(out=codes[:].bitcast(FP8X4), scales=scales[:],
+                                  in_=grouped[:].rearrange("w v p j -> w (v p j)"))
 
-        def mask(t):
-            gm = state[("gm", t)]
-            hd = work.tile([P, P], F32)
-            nc.vector.tensor_tensor(
-                out=hd[:].rearrange("p (n g) -> p n g", g=GROUPS),
-                in0=gm[:, 0, :].rearrange("p (g n) -> p n g", g=GROUPS), in1=on_diag[:], op=ALU.mult)
-            state[("hd", t)] = hd
+        transposed = {}
+        grouped_of = {}
+        codes_of = {}
 
-        def regroup(t):
-            nc.tensor.matmul(state[("gm", t)][:, 1, 0:V], lhsT=state[("hd", t)][:], rhs=of_view[:],
-                             start=True, stop=True)
+        def transpose_step(t):
+            transposed[t] = transposes(transpose_psum, "transposed", [row_of(v, t) for v in range(V)])
 
-        def gram_stats(t):
-            nd, k = stats(t)
-            first = 0 if t < GRAM_LENGTHS else 1
-            nc.vector.tensor_copy(out=nd[:, V - 1 + first:2 * V - 1, k], in_=state[("gm", t)][:, 1, first:V])
-
-        def quantise(key, codes, scales):
-            gt = state[("gt", key)]
-            nc.vector.quantize_mx(
-                out=codes[:].bitcast(FP8X4),
-                scales=scales[:],
-                in_=gt[:].rearrange("w n p j -> w (n p j)"),
-            )
+        def copy_step(t):
+            grouped = work.tile([P, V, P, PACK], BF16, align_bytes=64)
+            second = nc.scalar.copy if t in SCALAR_COPIES else nc.vector.tensor_copy
+            copy_out(transposed[t], grouped, (nc.vector.tensor_copy, second))
+            grouped_of[t] = grouped
 
         def quantise_step(t):
             codes = held.tile([P, V * P], U32, align_bytes=64)
             scales = held.tile([P, V * P], U8, align_bytes=64)
-            quantise(t, codes, scales)
-            state[("cd", t)] = (codes, scales)
+            quantise(grouped_of[t], codes, scales)
+            codes_of[t] = (codes, scales)
 
-        def mx_pass(dst, codes, scales, v, m_lo, m_hi):
-            nc.tensor.matmul_mx(
-                out=dst,
-                lhsT=codes[:, P * v:P * v + P].bitcast(FP8X4),
-                lhsT_scale=scales[:, P * v:P * v + P],
-                rhs=mem_codes[:, Q * m_lo:Q * m_hi].bitcast(FP8X4),
-                rhs_scale=mem_scales[:, Q * m_lo:Q * m_hi],
-                start=True,
-                stop=True,
-            )
+        numbers = {}
 
-        def products(t):
-            codes, scales = state[("cd", t)]
-            mm = mm_psum.tile([P, 4, Q], F32)
-            mx_pass(mm[:].rearrange("p n q -> p (n q)")[:, 0:2 * Q], codes, scales, 0, 1, 3)
-            mx_pass(mm[:, 2, :], codes, scales, 1, 0, 1)
-            mx_pass(mm[:, 3, :], codes, scales, 2, 0, 1)
-            state[("ma", t)] = mm
-            mm = mm_psum.tile([P, 4, Q], F32)
-            mx_pass(mm[:, 0, :], codes, scales, 0, 3, 4)
-            mx_pass(mm[:, 2, :], codes, scales, 1, 2, 3)
-            mx_pass(mm[:, 3, :], codes, scales, 2, 1, 2)
-            mx_pass(mm[:, 1, :], codes, scales, 3, 0, 1)
-            state[("mb", t)] = mm
-
-        def exps(t):
-            ma, mb = state[("ma", t)], state[("mb", t)]
-            sc = state[("sc", t // OCT)]
-            r = k = t % OCT
-            if r == 0:
-                ot = opool.tile([P, NCOMBO, OCT, ROW], F32)
-                state[("o", t // OCT)] = ot
-            ot = state[("o", t // OCT)]
-            for combos, bank, columns, pair in (
-                (slice(1, 6, 4), ma, slice(1, 4, 2), 1), (slice(0, 4, 3), ma, slice(0, 3, 2), 0),
-                (slice(2, 8, 5), mb, slice(0, 2), 2), (slice(4, 7, 2), mb, slice(2, 4), 3),
-            ):
-                nc.scalar.activation(out=ot[:, combos, r, 1:ROW], in_=bank[:, columns, :], func=ACT.Exp,
-                                     scale=sc[:, pair, k:k + 1])
-                if t == NT - 1:
-                    store(NT - 1, NT, combos)
-
-        arrivals = FIRST_LOADS + tuple((t, t + QUAD) for t in range(FIRST_LOADS[-1][1], NT, QUAD))
-        square_queue = [(t, v) for lo, hi in arrivals for v in LOAD_ORDER for t in range(lo, hi)
-                        if v > 0 or t >= GRAM_LENGTHS]
-        dot_queue = [(t, n) for t in range(NT) for n in range(len(PAIRS)) if n == 3 or t >= GRAM_STEPS]
-
-        def stats(t):
+        def numbers_of(t):
             o = t // OCT
-            if ("nd", o) not in state:
-                nd = small.tile([P, 2 * V, OCT], F32)
-                rn = small.tile([P, V, OCT], F32)
-                sc = small.tile([P, len(PAIRS), OCT], F32)
-                state[("nd", o)], state[("rn", o)], state[("sc", o)] = nd, rn, sc
-            return state[("nd", o)], t % OCT
+            if o not in numbers:
+                stats = small.tile([P, 2 * V, OCT], F32)
+                inverse = small.tile([P, V, OCT], F32)
+                scale = small.tile([P, len(PAIRS), OCT], F32)
+                numbers[o] = (stats, inverse, scale)
+            return numbers[o]
 
-        def next_square():
+        square_queue = [(t, v) for first, end in FIRST_LOADS + LATER_LOADS for v in LOAD_ORDER
+                        for t in range(first, end) if v > 0 or t >= GRAM_LENGTHS]
+        dot_queue = [(t, n) for t in range(STEPS) for n in range(len(PAIRS)) if n == 3 or t >= GRAM_STEPS]
+
+        def row_dot(i, j, t, total):
+            product = unread.tile([P, D], BF16)
+            nc.vector.scalar_tensor_tensor(out=product[:], in0=row_of(i, t), scalar=1.0, in1=row_of(j, t),
+                                           op0=ALU.mult, op1=ALU.mult, accum_out=total)
+
+        def next_square(on_vector=False):
             t, v = square_queue.pop(0)
-            nd, k = stats(t)
-            row = (v - 1) % V
-            if len(square_queue) % SHARED == 1:
-                jv = junk.tile([P, D], BF16)
-                nc.vector.scalar_tensor_tensor(
-                    out=jv[:], in0=row_of(v, t), scalar=1.0, in1=row_of(v, t),
-                    op0=ALU.mult, op1=ALU.mult, accum_out=nd[:, row, k:k + 1],
-                )
+            stats = numbers_of(t)[0]
+            total = stats[:, (v - 1) % V, t % OCT:t % OCT + 1]
+            if on_vector:
+                row_dot(v, v, t, total)
             else:
-                js = junk.tile([P, D], BF16)
-                nc.scalar.activation(out=js[:], in_=row_of(v, t), func=ACT.Square, accum_out=nd[:, row, k:k + 1])
+                square = unread.tile([P, D], BF16)
+                nc.scalar.activation(out=square[:], in_=row_of(v, t), func=ACT.Square, accum_out=total)
 
         def next_dot():
             t, n = dot_queue.pop(0)
-            nd, k = stats(t)
-            i, j = PAIRS[n]
-            jv = junk.tile([P, D], BF16)
-            nc.vector.scalar_tensor_tensor(
-                out=jv[:], in0=row_of(i, t), scalar=1.0, in1=row_of(j, t),
-                op0=ALU.mult, op1=ALU.mult, accum_out=nd[:, V + n, k:k + 1],
-            )
+            stats = numbers_of(t)[0]
+            row_dot(PAIRS[n][0], PAIRS[n][1], t, stats[:, V + n, t % OCT:t % OCT + 1])
 
-        def lengths_of(b):
-            lo, hi = BATCHES[b]
-            nd, k = stats(lo)
-            w = hi - lo
-            nc.gpsimd.tensor_tensor(out=state[("rn", lo // OCT)][:, :, k:k + w], in0=nd[:, 0:V, k:k + w],
-                                    in1=neg_half[:, :, 0:w], op=ALU.pow)
+        gram_of = {}
+        masked_of = {}
 
-        def scales_of(b):
-            lo, hi = BATCHES[b]
-            w, k, o = hi - lo, lo % OCT, lo // OCT
-            y = state[("rn", o)][:, :, k:k + w]
-            sc = state[("sc", o)]
+        def gram(t):
+            columns = grouped_of[t][:].rearrange("w v p j -> w (v p) j")
+            block = gram_psum.tile([P, 4, P], F32)
+            for g in range(GROUPS):
+                for j in range(PACK):
+                    nc.tensor.matmul(block[:, 0, GROUP * g:GROUP * g + GROUP], lhsT=columns[:, g:V * P:GROUPS, j],
+                                     rhs=columns[:, g:P:GROUPS, j], start=(j == 0), stop=(j == PACK - 1))
+            gram_of[t] = block
 
-            nc.vector.scalar_tensor_tensor(
-                out=sc[:, 0:3, k:k + w], in0=y[:, 0:3, :], scalar=1.0 / TEMP,
-                in1=y[:, 3:4, :].to_broadcast([P, 3, w]), op0=ALU.mult, op1=ALU.mult)
-            nc.vector.scalar_tensor_tensor(out=sc[:, 3, k:k + w], in0=y[:, 0, :], scalar=1.0 / TEMP,
+        def mask(t):
+            masked = work.tile([P, P], F32)
+            nc.vector.tensor_tensor(
+                out=masked[:].rearrange("p (n g) -> p n g", g=GROUPS),
+                in0=gram_of[t][:, 0, :].rearrange("p (g n) -> p n g", g=GROUPS), in1=on_diagonal[:], op=ALU.mult)
+            masked_of[t] = masked
+
+        def regroup(t):
+            nc.tensor.matmul(gram_of[t][:, 1, 0:V], lhsT=masked_of[t][:], rhs=of_view[:], start=True, stop=True)
+
+        def gram_numbers(t):
+            stats = numbers_of(t)[0]
+            first = 0 if t < GRAM_LENGTHS else 1
+            nc.vector.tensor_copy(out=stats[:, V - 1 + first:2 * V - 1, t % OCT], in_=gram_of[t][:, 1, first:V])
+
+        def inverses(t):
+            stats, inverse, scale = numbers_of(t)
+            k = t % OCT
+            nc.gpsimd.tensor_tensor(out=inverse[:, :, k:k + QUAD], in0=stats[:, 0:V, k:k + QUAD],
+                                    in1=neg_half[:, :, 0:QUAD], op=ALU.pow)
+
+        def scales_of(t):
+            stats, inverse, scale = numbers_of(t)
+            k = t % OCT
+            y = inverse[:, :, k:k + QUAD]
+            nc.vector.scalar_tensor_tensor(out=scale[:, 0:3, k:k + QUAD], in0=y[:, 0:3, :], scalar=1.0 / TEMP,
+                                           in1=y[:, 3:4, :].to_broadcast([P, 3, QUAD]), op0=ALU.mult, op1=ALU.mult)
+            nc.vector.scalar_tensor_tensor(out=scale[:, 3, k:k + QUAD], in0=y[:, 0, :], scalar=1.0 / TEMP,
                                            in1=y[:, 1, :], op0=ALU.mult, op1=ALU.mult)
 
-        def cosines(c):
-            lo, hi = COLUMNS[c]
-            o, k, w = lo // OCT, lo % OCT, hi - lo
-            zz = small.tile([P, len(PAIRS), OCT], F32)
-            nc.vector.tensor_tensor(out=zz[:, :, 0:w], in0=state[("nd", o)][:, V:2 * V, k:k + w],
-                                    in1=state[("sc", o)][:, :, k:k + w], op=ALU.mult)
-            state[("z", c)] = zz
+        products_of = {}
+        out_tiles = {}
+        cosines_of = {}
 
-        def first_column(c):
-            lo, hi = COLUMNS[c]
-            r, w = lo % OCT, hi - lo
-            zz = state[("z", c)]
-            ot = state[("o", lo // OCT)]
-            nc.scalar.activation(out=ot[:, 0:3, r:r + w, 0], in_=zz[:, 0:3, 0:w], func=ACT.Exp)
-            nc.scalar.activation(out=ot[:, 3:8:2, r:r + w, 0], in_=zz[:, 0:3, 0:w], func=ACT.Exp)
-            nc.scalar.activation(out=ot[:, 4:7:2, r:r + w, 0],
-                                 in_=zz[:, 3:4, 0:w].to_broadcast([P, 2, w]), func=ACT.Exp)
-
-        def store(lo, hi, combos=slice(0, NCOMBO)):
-            o = lo // OCT
-            ot = state[("o", o)]
-            first = Q * (lo - o * OCT)
-            end = OCT * ROW if hi == (o + 1) * OCT else Q * (hi - o * OCT)
-            nc.sync.dma_start(
-                out=out_view[:, combos, o * OCT * ROW + first:o * OCT * ROW + end],
-                in_=ot[:].rearrange("p c t q -> p c (t q)")[:, combos, first:end],
+        def mx_pass(dst, codes, scales, v, first_memory, end_memory):
+            columns = slice(Q * first_memory, Q * end_memory)
+            nc.tensor.matmul_mx(
+                out=dst,
+                lhsT=codes[:, P * v:P * v + P].bitcast(FP8X4), lhsT_scale=scales[:, P * v:P * v + P],
+                rhs=memory_codes[:, columns].bitcast(FP8X4), rhs_scale=memory_scales[:, columns],
+                start=True, stop=True,
             )
 
-        transposes(0, [row_of(v, 0).bitcast(F32) for v in range(V)])
-        batches_due = list(range(len(BATCHES)))
-        for n in range(max(SQUARES_AHEAD, DOTS_AHEAD)):
-            if n < SQUARES_AHEAD:
-                next_square()
-            if n < DOTS_AHEAD:
-                next_dot()
+        def products(t, second_pool, second_name):
+            codes, scales = codes_of[t]
+            product = product_psum.tile([P, 4, Q], F32)
+            mx_pass(product[:].rearrange("p n q -> p (n q)")[:, 0:2 * Q], codes, scales, 0, 1, 3)
+            mx_pass(product[:, 2, :], codes, scales, 1, 0, 1)
+            mx_pass(product[:, 3, :], codes, scales, 2, 0, 1)
+            second = second_pool.tile([P, 4, Q], F32, name=second_name)
+            mx_pass(second[:, 0, :], codes, scales, 0, 3, 4)
+            mx_pass(second[:, 2, :], codes, scales, 1, 2, 3)
+            mx_pass(second[:, 3, :], codes, scales, 2, 1, 2)
+            mx_pass(second[:, 1, :], codes, scales, 3, 0, 1)
+            products_of[t] = (product, second)
 
-        columns_due = list(range(len(COLUMNS)))
-        cosines_due = list(range(len(COLUMNS)))
+        def exps(t):
+            first, second = products_of[t]
+            scale = numbers_of(t)[2]
+            r = t % OCT
+            if r == 0:
+                out_tile = out_pool.tile([P, COMBOS, OCT, ROW], F32)
+                out_tiles[t // OCT] = out_tile
+            out_tile = out_tiles[t // OCT]
+            for combos, bank, columns, n in (
+                (slice(1, 6, 4), first, slice(1, 4, 2), 1), (slice(0, 4, 3), first, slice(0, 3, 2), 0),
+                (slice(2, 8, 5), second, slice(0, 2), 2), (slice(4, 7, 2), second, slice(2, 4), 3),
+            ):
+                nc.scalar.activation(out=out_tile[:, combos, r, 1:ROW], in_=bank[:, columns, :], func=ACT.Exp,
+                                     scale=scale[:, n, r:r + 1])
+                if t == STEPS - 1:
+                    store(STEPS - 1, STEPS, combos)
+
+        def cosines(first, end):
+            stats, inverse, scale = numbers_of(first)
+            k, w = first % OCT, end - first
+            cosine = small.tile([P, len(PAIRS), OCT], F32)
+            nc.vector.tensor_tensor(out=cosine[:, :, 0:w], in0=stats[:, V:2 * V, k:k + w], in1=scale[:, :, k:k + w],
+                                    op=ALU.mult)
+            cosines_of[first] = cosine
+
+        def first_column(first, end):
+            r, w = first % OCT, end - first
+            cosine = cosines_of[first]
+            column = out_tiles[first // OCT][:, :, r:r + w, 0]
+            nc.scalar.activation(out=column[:, 0:3, :], in_=cosine[:, 0:3, 0:w], func=ACT.Exp)
+            nc.scalar.activation(out=column[:, 3:8:2, :], in_=cosine[:, 0:3, 0:w], func=ACT.Exp)
+            nc.scalar.activation(out=column[:, 4:7:2, :], in_=cosine[:, 3:4, 0:w].to_broadcast([P, 2, w]),
+                                 func=ACT.Exp)
+
+        def store(first, end, combos=slice(0, COMBOS)):
+            o = first // OCT
+            lo = Q * (first - o * OCT)
+            hi = OCT * ROW if end == (o + 1) * OCT else Q * (end - o * OCT)
+            nc.sync.dma_start(out=out_view[:, combos, o * OCT * ROW + lo:o * OCT * ROW + hi],
+                              in_=out_tiles[o][:].rearrange("p c t q -> p c (t q)")[:, combos, lo:hi])
+
+        transpose_step(0)
+        for n in range(SQUARES_AHEAD):
+            next_square()
+        for n in range(DOTS_AHEAD):
+            next_dot()
+
+        quads_due = list(range(0, STEPS, QUAD))
+        scales_due = []
+        cosines_due = list(COLUMNS)
+        columns_due = list(COLUMNS)
         stores_due = list(STORES)
-        columns_done = 0
         scaled = 0
         multiplied = 0
         done = 0
+        column_end = 0
         i = 0
-        scales_due = []
-        while done < NT:
-            if i % QUAD == 1 and X_QUADS + i // QUAD - 1 in range(X_QUADS, NT // QUAD):
-                load(QUAD * (X_QUADS + i // QUAD - 1), QUAD * (X_QUADS + i // QUAD))
-            if i < NT:
-                copy_out(i, (i in SCALAR_FIRST, i in SCALAR_SECOND))
+        while done < STEPS:
+            q = X_QUADS + i // QUAD - 1
+            if i % QUAD == 1 and X_QUADS <= q < STEPS // QUAD:
+                load(QUAD * q, QUAD * q + QUAD)
+            if i < STEPS:
+                copy_step(i)
             if 0 <= i - 2 < GRAM_STEPS:
-                gram_stats(i - 2)
-            if i + 1 < NT:
-                transposes(i + 1, [row_of(v, i + 1).bitcast(F32) for v in range(V)])
+                gram_numbers(i - 2)
+            if i + 1 < STEPS:
+                transpose_step(i + 1)
             if i < GRAM_STEPS:
                 gram(i)
-            if 0 <= i - 1 < NT:
+            if 0 <= i - 1 < STEPS:
                 quantise_step(i - 1)
-                if i - 1 < GRAM_STEPS:
-                    mask(i - 1)
-                    regroup(i - 1)
+            if 0 <= i - 1 < GRAM_STEPS:
+                mask(i - 1)
+                regroup(i - 1)
             while scales_due and scales_due[0][0] == i:
-                b = scales_due.pop(0)[1]
-                scales_of(b)
-                scaled = BATCHES[b][1]
-            with_exps = False
-            for n in range(0 if i < EXPS_FROM else 1 if i < CATCH_UP else 2):
-                if PRE:
-                    if done < multiplied:
-                        exps(done)
-                        done += 1
-                        with_exps = True
-                    if multiplied < min(i - 1, scaled) and multiplied < done + 1:
-                        products(multiplied)
-                        multiplied += 1
-                elif done < min(i - 1, scaled):
-                    products(done)
+                t = scales_due.pop(0)[1]
+                scales_of(t)
+                scaled = t + QUAD
+
+            before = done
+            for n in range(0 if i < EXPS_FROM else 1 if i < TWO_EXPS_FROM else 2):
+                if done < multiplied:
                     exps(done)
                     done += 1
-                    with_exps = True
-            while columns_due and ("z", columns_due[0]) in state and COLUMNS[columns_due[0]][0] < done:
-                c = columns_due.pop(0)
-                first_column(c)
-                columns_done = COLUMNS[c][1]
-            while stores_due and stores_due[0][1] <= min(done, columns_done):
+                spare = i > GRAM_STEPS
+                if multiplied < min(i - 1, scaled, done + (2 if spare else 1)):
+                    products(multiplied, *((gram_psum, "block") if spare else (product_psum, "product")))
+                    multiplied += 1
+            while columns_due and columns_due[0][0] in cosines_of and columns_due[0][0] < done:
+                first, end = columns_due.pop(0)
+                first_column(first, end)
+                column_end = end
+            while stores_due and stores_due[0][1] <= min(done, column_end):
                 store(*stores_due.pop(0))
-            squared_before = min([t for t, v in square_queue] + [NT])
-            quarters = SQUARES_BESIDE if with_exps else SQUARES_ALONE
-            for n in range((i + 1) * quarters // 4 - i * quarters // 4):
+
+            squared = min([t for t, v in square_queue] + [STEPS])
+            in_two = SQUARES_BESIDE if done > before else SQUARES_ALONE
+            for n in range((i + 1) * in_two // 2 - i * in_two // 2):
                 if square_queue:
-                    next_square()
+                    next_square(done > before and i % VECTOR_SQUARE == 0 and n == 0)
             if i < GRAM_STEPS:
-                dots = (i + 1) * DOT_QUARTERS // 4 - i * DOT_QUARTERS // 4
+                dots = (i + 1) * DOTS_IN_TWO // 2 - i * DOTS_IN_TWO // 2
             else:
                 dots = share(len(dot_queue), DOTS_END - i)
             for n in range(min(dots, len(dot_queue))):
                 next_dot()
-            if i == MEM_STEP:
-                mem_words = mem_nat[:].bitcast(F32)
-                transposes("mem", [mem_words[:, j, :] for j in range(V)])
-            if i == MEM_STEP + 1:
-                copy_out("mem", (False, False))
-            if i == MEM_STEP + 2:
-                quantise("mem", mem_codes, mem_scales)
-            dotted = dot_queue[0][0] if dot_queue else NT
-            while cosines_due and COLUMNS[cosines_due[0]][1] <= min(scaled, dotted) and (
-                    i - 2 >= min(COLUMNS[cosines_due[0]][1], GRAM_STEPS) - 1):
-                cosines(cosines_due.pop(0))
-            if batches_due:
-                lo, hi = BATCHES[batches_due[0]]
-                last = min(hi, GRAM_LENGTHS) - 1
-                if squared_before >= hi and (lo >= GRAM_LENGTHS or i - 2 >= last):
-                    b = batches_due.pop(0)
-                    lengths_of(b)
-                    scales_due.append((i + SCALE_DELAY, b))
+
+            if i == MEMORY_STEP:
+                memory_banks = transposes(product_psum, "product", [memory_rows[:, j, :] for j in range(V)])
+            if i == MEMORY_STEP + 1:
+                memory_grouped = keep.tile([P, V, P, PACK], BF16, name="memory_grouped", align_bytes=64)
+                copy_out(memory_banks, memory_grouped, (nc.vector.tensor_copy, nc.vector.tensor_copy))
+            if i == MEMORY_STEP + 2:
+                quantise(memory_grouped, memory_codes, memory_scales)
+
+            dotted = dot_queue[0][0] if dot_queue else STEPS
+            while cosines_due and cosines_due[0][1] <= min(scaled, dotted) and (
+                    i - 2 >= min(cosines_due[0][1], GRAM_STEPS) - 1):
+                cosines(*cosines_due.pop(0))
+            if quads_due:
+                t = quads_due[0]
+                if squared >= t + QUAD and (t >= GRAM_LENGTHS or i - 2 >= min(t + QUAD, GRAM_LENGTHS) - 1):
+                    inverses(quads_due.pop(0))
+                    scales_due.append((i + SCALES_AFTER, t))
             i += 1

from contextlib import ExitStack

import concourse.mybir as mybir
from concourse.masks import make_identity

BF16 = mybir.dt.bfloat16
F32 = mybir.dt.float32
U32 = mybir.dt.uint32
U8 = mybir.dt.uint8
FP8X4 = mybir.dt.float8_e4m3fn_x4
ACT = mybir.ActivationFunctionType
ALU = mybir.AluOpType

P = 128
B, Q, D = 4096, 128, 512
V = 4
STEPS = B // P
TEMP = 0.07
COMBOS = 8
ROW = Q + 1
PACK = 4
QUAD = 4
OCT = 8
PAIRS = ((0, 1), (0, 2), (0, 3), (1, 2))

GROUPS = 4
GROUP = P // GROUPS
GRAM_STEPS = 25
GRAM_LENGTHS = 21

FIRST_LOADS = ((0, 1), (1, 2), (2, 4), (4, 8))
LATER_LOADS = tuple((t, t + QUAD) for t in range(FIRST_LOADS[-1][1], STEPS, QUAD))
LOAD_ORDER = (1, 0, 2, 3)
X_QUADS = 6
HELD = 11

SQUARES_AHEAD = 12
SQUARES_ALONE = 9
SQUARES_BESIDE = 7
VECTOR_SQUARE = 4
DOTS_AHEAD = 1
DOTS_IN_TWO = 3
DOTS_END = 31
EXPS_FROM = 7
TWO_EXPS_FROM = 24
MEMORY_STEP = 2
SCALAR_COPIES = range(28, 31)
SCALES_AFTER = 2

COLUMNS = ((0, 8), (8, 16), (16, 20), (20, 24), (24, 28), (28, 30), (30, 32))
STORES = ((0, 8), (8, 12), (12, 16), (16, 20), (20, 22), (22, 24), (24, 26), (26, 28), (28, 29), (29, 30), (30, 31))

FLOPS = 2 * COMBOS * B * ROW * D


def share(left, steps):
    return -(-left // steps) if steps > 0 else left


def tile_memorymoco_pa_t_kernel(tc, x0, x1, x2, x3, mem0, mem1, mem2, mem3, out):
    nc = tc.nc
    views = [x.rearrange("(p t) d -> p t d", t=STEPS) for x in (x0, x1, x2, x3)]
    memories = (mem0, mem1, mem2, mem3)
    out_view = out.rearrange("c (p t) q -> p c (t q)", t=STEPS)

    with ExitStack() as ctx:
        keep = ctx.enter_context(tc.tile_pool(name="keep", bufs=1))
        row_pool = ctx.enter_context(tc.tile_pool(name="row_pool", bufs=X_QUADS))
        out_pool = ctx.enter_context(tc.tile_pool(name="out_pool", bufs=2))
        work = ctx.enter_context(tc.tile_pool(name="work", bufs=3))
        held = ctx.enter_context(tc.tile_pool(name="held", bufs=HELD))
        unread = ctx.enter_context(tc.tile_pool(name="unread", bufs=2))
        small = ctx.enter_context(tc.tile_pool(name="small", bufs=4))
        transpose_psum = ctx.enter_context(tc.psum_pool(name="transpose_psum", bufs=3))
        gram_psum = ctx.enter_context(tc.psum_pool(name="gram_psum", bufs=2))
        product_psum = ctx.enter_context(tc.psum_pool(name="product_psum", bufs=3))
        ctx.enter_context(tc.manual_schedule())

        memory_rows = keep.tile([P, V, D], BF16, name="memory_rows")
        quads = {}

        def load(first, end):
            for v in LOAD_ORDER:
                q = first // QUAD
                if first % QUAD == 0:
                    rows = row_pool.tile([P, QUAD, D], BF16, name="rows%d" % v)
                    quads[(v, q)] = rows
                nc.sync.dma_start(out=quads[(v, q)][:, first - QUAD * q:end - QUAD * q, :],
                                  in_=views[v][:, first:end, :])

        def row_of(v, t):
            return quads[(v, t // QUAD)][:, t % QUAD, :]

        for first, end in FIRST_LOADS:
            load(first, end)
        for j in range(V):
            nc.sync.dma_start(out=memory_rows[:, j, :], in_=memories[j])
        for first, end in LATER_LOADS[:X_QUADS - FIRST_LOADS[-1][1] // QUAD]:
            load(first, end)

        ident = keep.tile([P, P], F32, name="ident")
        make_identity(nc, ident[:])
        of_view = keep.tile([P, V], F32, name="of_view")
        nc.vector.tensor_reduce(out=of_view[:], in_=ident[:].rearrange("p (v r) -> p v r", v=V),
                                axis=mybir.AxisListType.X, op=ALU.add)
        of_row = keep.tile([P, GROUP], F32, name="of_row")
        nc.vector.tensor_reduce(out=of_row[:], in_=ident[:].rearrange("p (v r) -> p r v", v=V),
                                axis=mybir.AxisListType.X, op=ALU.add)
        on_diagonal = keep.tile([P, GROUP, GROUPS], F32, name="on_diagonal")
        nc.vector.tensor_copy(out=on_diagonal[:], in_=of_row[:].unsqueeze(2).to_broadcast([P, GROUP, GROUPS]))
        neg_half = keep.tile([P, V, OCT], F32, name="neg_half")
        nc.gpsimd.memset(neg_half[:], -0.5)
        warm_in = keep.tile([P, 1], F32, name="warm_in")
        warm_out = keep.tile([P, 1], F32, name="warm_out")
        nc.vector.memset(warm_in[:], 0.0)
        nc.scalar.activation(out=warm_out[:], in_=warm_in[:], func=ACT.Exp)

        memory_codes = keep.tile([P, V * Q], U32, name="memory_codes", align_bytes=64)
        memory_scales = keep.tile([P, V * Q], U8, name="memory_scales", align_bytes=64)

        def transposes(pool, name, sources):
            banks = []
            for h in range(2):
                bank = pool.tile([P, 2, 2, P], F32, name=name)
                for v in (2 * h, 2 * h + 1):
                    for u in range(2):
                        nc.tensor.transpose(bank[:, v % 2, u, :], sources[v].bitcast(F32)[:, u:2 * P:2], ident[:])
                banks.append(bank)
            return banks

        def copy_out(banks, grouped, engines):
            words = grouped[:].bitcast(F32)
            for h in range(2):
                engines[h](out=words[:, 2 * h:2 * h + 2, :, :], in_=banks[h][:].rearrange("w n u p -> w n p u"))

        def quantise(grouped, codes, scales):
            nc.vector.quantize_mx(out=codes[:].bitcast(FP8X4), scales=scales[:],
                                  in_=grouped[:].rearrange("w v p j -> w (v p j)"))

        transposed = {}
        grouped_of = {}
        codes_of = {}

        def transpose_step(t):
            transposed[t] = transposes(transpose_psum, "transposed", [row_of(v, t) for v in range(V)])

        def copy_step(t):
            grouped = work.tile([P, V, P, PACK], BF16, align_bytes=64)
            second = nc.scalar.copy if t in SCALAR_COPIES else nc.vector.tensor_copy
            copy_out(transposed[t], grouped, (nc.vector.tensor_copy, second))
            grouped_of[t] = grouped

        def quantise_step(t):
            codes = held.tile([P, V * P], U32, align_bytes=64)
            scales = held.tile([P, V * P], U8, align_bytes=64)
            quantise(grouped_of[t], codes, scales)
            codes_of[t] = (codes, scales)

        numbers = {}

        def numbers_of(t):
            o = t // OCT
            if o not in numbers:
                stats = small.tile([P, 2 * V, OCT], F32)
                inverse = small.tile([P, V, OCT], F32)
                scale = small.tile([P, len(PAIRS), OCT], F32)
                numbers[o] = (stats, inverse, scale)
            return numbers[o]

        square_queue = [(t, v) for first, end in FIRST_LOADS + LATER_LOADS for v in LOAD_ORDER
                        for t in range(first, end) if v > 0 or t >= GRAM_LENGTHS]
        dot_queue = [(t, n) for t in range(STEPS) for n in range(len(PAIRS)) if n == 3 or t >= GRAM_STEPS]

        def row_dot(i, j, t, total):
            product = unread.tile([P, D], BF16)
            nc.vector.scalar_tensor_tensor(out=product[:], in0=row_of(i, t), scalar=1.0, in1=row_of(j, t),
                                           op0=ALU.mult, op1=ALU.mult, accum_out=total)

        def next_square(on_vector=False):
            t, v = square_queue.pop(0)
            stats = numbers_of(t)[0]
            total = stats[:, (v - 1) % V, t % OCT:t % OCT + 1]
            if on_vector:
                row_dot(v, v, t, total)
            else:
                square = unread.tile([P, D], BF16)
                nc.scalar.activation(out=square[:], in_=row_of(v, t), func=ACT.Square, accum_out=total)

        def next_dot():
            t, n = dot_queue.pop(0)
            stats = numbers_of(t)[0]
            row_dot(PAIRS[n][0], PAIRS[n][1], t, stats[:, V + n, t % OCT:t % OCT + 1])

        gram_of = {}
        masked_of = {}

        def gram(t):
            columns = grouped_of[t][:].rearrange("w v p j -> w (v p) j")
            block = gram_psum.tile([P, 4, P], F32)
            for g in range(GROUPS):
                for j in range(PACK):
                    nc.tensor.matmul(block[:, 0, GROUP * g:GROUP * g + GROUP], lhsT=columns[:, g:V * P:GROUPS, j],
                                     rhs=columns[:, g:P:GROUPS, j], start=(j == 0), stop=(j == PACK - 1))
            gram_of[t] = block

        def mask(t):
            masked = work.tile([P, P], F32)
            nc.vector.tensor_tensor(
                out=masked[:].rearrange("p (n g) -> p n g", g=GROUPS),
                in0=gram_of[t][:, 0, :].rearrange("p (g n) -> p n g", g=GROUPS), in1=on_diagonal[:], op=ALU.mult)
            masked_of[t] = masked

        def regroup(t):
            nc.tensor.matmul(gram_of[t][:, 1, 0:V], lhsT=masked_of[t][:], rhs=of_view[:], start=True, stop=True)

        def gram_numbers(t):
            stats = numbers_of(t)[0]
            first = 0 if t < GRAM_LENGTHS else 1
            nc.vector.tensor_copy(out=stats[:, V - 1 + first:2 * V - 1, t % OCT], in_=gram_of[t][:, 1, first:V])

        def inverses(t):
            stats, inverse, scale = numbers_of(t)
            k = t % OCT
            nc.gpsimd.tensor_tensor(out=inverse[:, :, k:k + QUAD], in0=stats[:, 0:V, k:k + QUAD],
                                    in1=neg_half[:, :, 0:QUAD], op=ALU.pow)

        def scales_of(t):
            stats, inverse, scale = numbers_of(t)
            k = t % OCT
            y = inverse[:, :, k:k + QUAD]
            nc.vector.scalar_tensor_tensor(out=scale[:, 0:3, k:k + QUAD], in0=y[:, 0:3, :], scalar=1.0 / TEMP,
                                           in1=y[:, 3:4, :].to_broadcast([P, 3, QUAD]), op0=ALU.mult, op1=ALU.mult)
            nc.vector.scalar_tensor_tensor(out=scale[:, 3, k:k + QUAD], in0=y[:, 0, :], scalar=1.0 / TEMP,
                                           in1=y[:, 1, :], op0=ALU.mult, op1=ALU.mult)

        products_of = {}
        out_tiles = {}
        cosines_of = {}

        def mx_pass(dst, codes, scales, v, first_memory, end_memory):
            columns = slice(Q * first_memory, Q * end_memory)
            nc.tensor.matmul_mx(
                out=dst,
                lhsT=codes[:, P * v:P * v + P].bitcast(FP8X4), lhsT_scale=scales[:, P * v:P * v + P],
                rhs=memory_codes[:, columns].bitcast(FP8X4), rhs_scale=memory_scales[:, columns],
                start=True, stop=True,
            )

        def products(t, second_pool, second_name):
            codes, scales = codes_of[t]
            product = product_psum.tile([P, 4, Q], F32)
            mx_pass(product[:].rearrange("p n q -> p (n q)")[:, 0:2 * Q], codes, scales, 0, 1, 3)
            mx_pass(product[:, 2, :], codes, scales, 1, 0, 1)
            mx_pass(product[:, 3, :], codes, scales, 2, 0, 1)
            second = second_pool.tile([P, 4, Q], F32, name=second_name)
            mx_pass(second[:, 0, :], codes, scales, 0, 3, 4)
            mx_pass(second[:, 2, :], codes, scales, 1, 2, 3)
            mx_pass(second[:, 3, :], codes, scales, 2, 1, 2)
            mx_pass(second[:, 1, :], codes, scales, 3, 0, 1)
            products_of[t] = (product, second)

        def exps(t):
            first, second = products_of[t]
            scale = numbers_of(t)[2]
            r = t % OCT
            if r == 0:
                out_tile = out_pool.tile([P, COMBOS, OCT, ROW], F32)
                out_tiles[t // OCT] = out_tile
            out_tile = out_tiles[t // OCT]
            for combos, bank, columns, n in (
                (slice(1, 6, 4), first, slice(1, 4, 2), 1), (slice(0, 4, 3), first, slice(0, 3, 2), 0),
                (slice(2, 8, 5), second, slice(0, 2), 2), (slice(4, 7, 2), second, slice(2, 4), 3),
            ):
                nc.scalar.activation(out=out_tile[:, combos, r, 1:ROW], in_=bank[:, columns, :], func=ACT.Exp,
                                     scale=scale[:, n, r:r + 1])
                if t == STEPS - 1:
                    store(STEPS - 1, STEPS, combos)

        def cosines(first, end):
            stats, inverse, scale = numbers_of(first)
            k, w = first % OCT, end - first
            cosine = small.tile([P, len(PAIRS), OCT], F32)
            nc.vector.tensor_tensor(out=cosine[:, :, 0:w], in0=stats[:, V:2 * V, k:k + w], in1=scale[:, :, k:k + w],
                                    op=ALU.mult)
            cosines_of[first] = cosine

        def first_column(first, end):
            r, w = first % OCT, end - first
            cosine = cosines_of[first]
            column = out_tiles[first // OCT][:, :, r:r + w, 0]
            nc.scalar.activation(out=column[:, 0:3, :], in_=cosine[:, 0:3, 0:w], func=ACT.Exp)
            nc.scalar.activation(out=column[:, 3:8:2, :], in_=cosine[:, 0:3, 0:w], func=ACT.Exp)
            nc.scalar.activation(out=column[:, 4:7:2, :], in_=cosine[:, 3:4, 0:w].to_broadcast([P, 2, w]),
                                 func=ACT.Exp)

        def store(first, end, combos=slice(0, COMBOS)):
            o = first // OCT
            lo = Q * (first - o * OCT)
            hi = OCT * ROW if end == (o + 1) * OCT else Q * (end - o * OCT)
            nc.sync.dma_start(out=out_view[:, combos, o * OCT * ROW + lo:o * OCT * ROW + hi],
                              in_=out_tiles[o][:].rearrange("p c t q -> p c (t q)")[:, combos, lo:hi])

        transpose_step(0)
        for n in range(SQUARES_AHEAD):
            next_square()
        for n in range(DOTS_AHEAD):
            next_dot()

        quads_due = list(range(0, STEPS, QUAD))
        scales_due = []
        cosines_due = list(COLUMNS)
        columns_due = list(COLUMNS)
        stores_due = list(STORES)
        scaled = 0
        multiplied = 0
        done = 0
        column_end = 0
        i = 0
        while done < STEPS:
            q = X_QUADS + i // QUAD - 1
            if i % QUAD == 1 and X_QUADS <= q < STEPS // QUAD:
                load(QUAD * q, QUAD * q + QUAD)
            if i < STEPS:
                copy_step(i)
            if 0 <= i - 2 < GRAM_STEPS:
                gram_numbers(i - 2)
            if i + 1 < STEPS:
                transpose_step(i + 1)
            if i < GRAM_STEPS:
                gram(i)
            if 0 <= i - 1 < STEPS:
                quantise_step(i - 1)
            if 0 <= i - 1 < GRAM_STEPS:
                mask(i - 1)
                regroup(i - 1)
            while scales_due and scales_due[0][0] == i:
                t = scales_due.pop(0)[1]
                scales_of(t)
                scaled = t + QUAD

            before = done
            for n in range(0 if i < EXPS_FROM else 1 if i < TWO_EXPS_FROM else 2):
                if done < multiplied:
                    exps(done)
                    done += 1
                spare = i > GRAM_STEPS
                if multiplied < min(i - 1, scaled, done + (2 if spare else 1)):
                    products(multiplied, *((gram_psum, "block") if spare else (product_psum, "product")))
                    multiplied += 1
            while columns_due and columns_due[0][0] in cosines_of and columns_due[0][0] < done:
                first, end = columns_due.pop(0)
                first_column(first, end)
                column_end = end
            while stores_due and stores_due[0][1] <= min(done, column_end):
                store(*stores_due.pop(0))

            squared = min([t for t, v in square_queue] + [STEPS])
            in_two = SQUARES_BESIDE if done > before else SQUARES_ALONE
            for n in range((i + 1) * in_two // 2 - i * in_two // 2):
                if square_queue:
                    next_square(done > before and i % VECTOR_SQUARE == 0 and n == 0)
            if i < GRAM_STEPS:
                dots = (i + 1) * DOTS_IN_TWO // 2 - i * DOTS_IN_TWO // 2
            else:
                dots = share(len(dot_queue), DOTS_END - i)
            for n in range(min(dots, len(dot_queue))):
                next_dot()

            if i == MEMORY_STEP:
                memory_banks = transposes(product_psum, "product", [memory_rows[:, j, :] for j in range(V)])
            if i == MEMORY_STEP + 1:
                memory_grouped = keep.tile([P, V, P, PACK], BF16, name="memory_grouped", align_bytes=64)
                copy_out(memory_banks, memory_grouped, (nc.vector.tensor_copy, nc.vector.tensor_copy))
            if i == MEMORY_STEP + 2:
                quantise(memory_grouped, memory_codes, memory_scales)

            dotted = dot_queue[0][0] if dot_queue else STEPS
            while cosines_due and cosines_due[0][1] <= min(scaled, dotted) and (
                    i - 2 >= min(cosines_due[0][1], GRAM_STEPS) - 1):
                cosines(*cosines_due.pop(0))
            if quads_due:
                t = quads_due[0]
                if squared >= t + QUAD and (t >= GRAM_LENGTHS or i - 2 >= min(t + QUAD, GRAM_LENGTHS) - 1):
                    inverses(quads_due.pop(0))
                    scales_due.append((i + SCALES_AFTER, t))
            i += 1
